import numpy as np
import ml_dtypes


def mxq(x, axis, fmt="e4m3"):
    dtype, down = {"e4m3": (ml_dtypes.float8_e4m3fn, 7), "e5m2": (ml_dtypes.float8_e5m2, 14)}[fmt]
    v = np.moveaxis(np.asarray(x, np.float32).astype(ml_dtypes.bfloat16).astype(np.float64), axis, -1)
    blocks = v.reshape(v.shape[:-1] + (-1, 32))
    amax = np.abs(blocks).max(-1, keepdims=True)
    byte = np.maximum(np.where(amax > 0, np.frexp(amax)[1] - 1 + 127, 0) - down, 1)
    scale = np.exp2(byte - 127.0)
    codes = (blocks / scale).astype(np.float32).astype(dtype).astype(np.float64)
    return np.moveaxis((codes * scale).reshape(v.shape), -1, axis)


WIDE = False


def mx_kscale(k):
    if not WIDE:
        return np.ones(k)
    levels = np.array([10, -10, 5, -5, 0])
    a = np.random.permutation(np.resize(levels, k // 512 * 4)).reshape(k // 512, 4)
    idx = np.arange(k)
    return np.exp2(a[idx // 512, idx % 128 // 32])


BF16 = ml_dtypes.bfloat16


def bf(x):
    return np.asarray(x, np.float32).astype(BF16)


def f64(x):
    return np.asarray(x).astype(np.float64)


B, S, HID, NH = 4, 2048, 512, 16
LN_EPS = 1e-5


def sigmoid(v):
    return 1.0 / (1.0 + np.exp(-v))


def setup_inputs():
    s = mx_kscale(HID)
    w = 1.0 / np.sqrt(HID)
    return {"hidden_states": bf(np.random.standard_normal((B, S, HID))),
            "attn_ctx": bf(np.random.standard_normal((B, S, HID)) * 0.3 * s),
            "Wo": bf(np.random.standard_normal((HID, HID)) * 3.0 * w / s[:, None]),
            "bo": bf(np.random.standard_normal(HID) * 0.3 + 0.3),
            "Wg": bf(np.random.standard_normal((HID, HID)) * w),
            "bg": bf(np.random.standard_normal(HID) * 0.5),
            "ln_gamma": bf(1.0 + 0.1 * np.random.standard_normal(HID)),
            "ln_beta": bf(0.1 * np.random.standard_normal(HID))}


def reference(hidden_states, attn_ctx, Wo, bo, Wg, bg, ln_gamma, ln_beta):
    h = f64(hidden_states)
    attn = (mxq(f64(attn_ctx), 2, "e4m3") @ mxq(f64(Wo), 0, "e4m3")) + f64(bo)
    gate = sigmoid((mxq(h, 2, "e4m3") @ mxq(f64(Wg), 0, "e4m3")) + f64(bg))
    y = h + gate * attn
    mu = y.mean(-1, keepdims=True)
    var = np.square(y - mu).mean(-1, keepdims=True)
    return (y - mu) / np.sqrt(var + LN_EPS) * f64(ln_gamma) + f64(ln_beta)

@@ -1,0 +1,251 @@
+from contextlib import ExitStack
+
+import concourse.mybir as mybir
+from concourse.masks import make_identity
+
+F32 = mybir.dt.float32
+BF16 = mybir.dt.bfloat16
+U32 = mybir.dt.uint32
+U8 = mybir.dt.uint8
+FP8X4 = mybir.dt.float8_e4m3fn_x4
+ACT = mybir.ActivationFunctionType
+ALU = mybir.AluOpType
+
+P = 128
+PACK = 4
+HID = 512
+TOKENS = 4 * 2048
+LN_EPS = 1e-5
+
+CHUNKS = HID // P
+TILES_PER_GROUP = 4
+GROUP = TILES_PER_GROUP * P
+N_GROUPS = TOKENS // GROUP
+N_TILES = TOKENS // P
+CTX, HS = 0, 1
+
+LAG_QUANTISE = 2
+LAG_PRODUCTS = 7
+LAG_RESIDUAL = 12
+LAG_CENTRE = 14
+LAG_SCALE = 16
+GROUPS_AHEAD = 2
+
+FLOPS = 2 * 2 * TOKENS * HID * HID
+
+
+def tile_crossattentionlayer_pa_t_kernel(
+    tc, hidden_states, attn_ctx, Wo, bo, Wg, bg, ln_gamma, ln_beta, out
+):
+    nc = tc.nc
+    by_group = "(g p j) k -> g p j k"
+    ctx_dram = attn_ctx.flatten_outer_dims().rearrange(by_group, p=P, j=TILES_PER_GROUP)
+    hs_dram = hidden_states.flatten_outer_dims().rearrange(by_group, p=P, j=TILES_PER_GROUP)
+    out_dram = out.flatten_outer_dims().rearrange(by_group, p=P, j=TILES_PER_GROUP)
+
+    with ExitStack() as stack:
+        consts = stack.enter_context(tc.tile_pool(name="consts", bufs=1))
+        loads = stack.enter_context(tc.tile_pool(name="loads", bufs=4))
+        work = stack.enter_context(tc.tile_pool(name="work", bufs=4))
+        stats = stack.enter_context(tc.tile_pool(name="stats", bufs=6))
+        psum = stack.enter_context(tc.psum_pool(name="psum", bufs=2))
+
+        def quantise_weight(w, label):
+            raw = consts.tile([P, PACK, HID], BF16, name=label + "_raw")
+            nc.sync.dma_start(
+                out=raw[:].rearrange("p (u e) f -> p u (e f)", u=2),
+                in_=w.rearrange("(u p e) f -> p u (e f)", u=2, p=P),
+            )
+            grouped = consts.tile([P, HID, PACK], BF16, name=label + "_grouped", align_bytes=64)
+            nc.vector.tensor_copy(out=grouped[:], in_=raw[:].rearrange("p t f -> p f t"))
+            w_codes = consts.tile([P, HID], U32, name=label + "_codes", align_bytes=64)
+            w_scales = consts.tile([P, HID], U8, name=label + "_scales", align_bytes=64)
+            nc.vector.quantize_mx(
+                out=w_codes[:].bitcast(FP8X4),
+                scales=w_scales[:],
+                in_=grouped[:].rearrange("p f t -> p (f t)"),
+            )
+            return w_codes, w_scales
+
+        wo_codes, wo_scales = quantise_weight(Wo, "wo")
+        wg_codes, wg_scales = quantise_weight(Wg, "wg")
+
+        ctx_nat = {}
+        hs_nat = {}
+
+        def load_group(g):
+            ctx_nat[g] = loads.tile([P, TILES_PER_GROUP, HID], BF16, name="ctx_nat", tag="ctx_nat")
+            nc.sync.dma_start(out=ctx_nat[g][:], in_=ctx_dram[g])
+            hs_nat[g] = loads.tile([P, TILES_PER_GROUP, HID], BF16, name="hs_nat", tag="hs_nat", bufs=7)
+            nc.sync.dma_start(out=hs_nat[g][:], in_=hs_dram[g])
+
+        for g in range(GROUPS_AHEAD):
+            load_group(g)
+
+        ident = consts.tile([P, P], F32, name="ident")
+        make_identity(nc, ident[:])
+        neg_half = consts.tile([P, 1], F32, name="neg_half")
+        nc.vector.memset(neg_half[:], -0.5)
+
+        gamma_rows = consts.tile([P, HID], BF16, name="gamma_rows")
+        nc.scalar.dma_start(out=gamma_rows[:], in_=ln_gamma.partition_broadcast(P))
+        beta_rows = consts.tile([P, HID], BF16, name="beta_rows")
+        nc.scalar.dma_start(out=beta_rows[:], in_=ln_beta.partition_broadcast(P))
+
+        bias_rows = consts.tile([P, P], BF16, name="bias_rows")
+        nc.vector.memset(bias_rows[:], 0.0)
+        nc.scalar.dma_start(out=bias_rows[0:CHUNKS, :], in_=bo.rearrange("(c f) -> c f", f=P))
+        nc.scalar.dma_start(out=bias_rows[CHUNKS : 2 * CHUNKS, :], in_=bg.rearrange("(c f) -> c f", f=P))
+        bias_rows_f32 = consts.tile([P, P], F32, name="bias_rows_f32")
+        nc.vector.tensor_copy(out=bias_rows_f32[:], in_=bias_rows[:])
+        bias_ps = psum.tile([P, P], F32, name="bias_ps", tag="words_ps")
+        nc.tensor.transpose(bias_ps[:], bias_rows_f32[:], ident[:])
+        bias_cols = consts.tile([P, 2 * CHUNKS], F32, name="bias_cols")
+        nc.vector.tensor_copy(out=bias_cols[:], in_=bias_ps[:, 0 : 2 * CHUNKS])
+
+        grouped = {}
+        codes = {}
+        scales = {}
+        gated_t = {}
+        y = {}
+        neg_mean = {}
+        centred = {}
+        rstd = {}
+
+        def transpose_tile(t):
+            g, j = divmod(t, TILES_PER_GROUP)
+            if j == 0:
+                grouped[g] = work.tile(
+                    [P, 2, GROUP, PACK], BF16, name="grouped", tag="grouped", bufs=2, align_bytes=64
+                )
+            words_ps = psum.tile([P, 2, 2, P], F32, name="words_ps", tag="words_ps")
+            for operand, nat in ((CTX, ctx_nat[g]), (HS, hs_nat[g])):
+                words = nat[:].bitcast(F32)
+                for u in range(2):
+                    nc.tensor.transpose(words_ps[:, operand, u, :], words[:, j, u * P : (u + 1) * P], ident[:])
+            nc.scalar.copy(
+                out=grouped[g][:].bitcast(F32)[:, :, j * P : (j + 1) * P, :],
+                in_=words_ps[:].rearrange("p o u r -> p o r u"),
+            )
+
+        def quantise_tile(t):
+            g, j = divmod(t, TILES_PER_GROUP)
+            if j == 0:
+                codes[g] = work.tile([P, 2, GROUP], U32, name="codes", tag="codes", bufs=3, align_bytes=64)
+                scales[g] = work.tile([P, 2, GROUP], U8, name="scales", tag="scales", bufs=3, align_bytes=64)
+            cols = slice(j * P, (j + 1) * P)
+            for operand in (CTX, HS):
+                nc.vector.quantize_mx(
+                    out=codes[g][:, operand, cols].bitcast(FP8X4),
+                    scales=scales[g][:, operand, cols],
+                    in_=grouped[g][:, operand, cols, :].rearrange("p r t -> p (r t)"),
+                )
+
+        def products_of_chunk(s):
+            g, c = divmod(s, CHUNKS)
+            if c == 0:
+                gated_t[g] = work.tile([P, CHUNKS, GROUP], F32, name="gated_t", tag="gated_t", bufs=3)
+            feats = slice(c * P, (c + 1) * P)
+            attn_ps = psum.tile([P, GROUP], F32, name="attn_ps", tag="attn_ps")
+            nc.tensor.matmul_mx(
+                out=attn_ps[:],
+                lhsT=wo_codes[:, feats].bitcast(FP8X4),
+                lhsT_scale=wo_scales[:, feats],
+                rhs=codes[g][:, CTX, :].bitcast(FP8X4),
+                rhs_scale=scales[g][:, CTX, :],
+                start=True,
+                stop=True,
+            )
+            gate_ps = psum.tile([P, GROUP], F32, name="gate_ps", tag="gate_ps")
+            nc.tensor.matmul_mx(
+                out=gate_ps[:],
+                lhsT=wg_codes[:, feats].bitcast(FP8X4),
+                lhsT_scale=wg_scales[:, feats],
+                rhs=codes[g][:, HS, :].bitcast(FP8X4),
+                rhs_scale=scales[g][:, HS, :],
+                start=True,
+                stop=True,
+            )
+            gate = work.tile([P, GROUP], F32, name="gate", tag="gate")
+            nc.scalar.activation(
+                out=gate[:], in_=gate_ps[:], func=ACT.Sigmoid, bias=bias_cols[:, CHUNKS + c : CHUNKS + c + 1], scale=1.0
+            )
+            nc.vector.scalar_tensor_tensor(
+                out=gated_t[g][:, c, :],
+                in0=attn_ps[:],
+                scalar=bias_cols[:, c : c + 1],
+                in1=gate[:],
+                op0=ALU.add,
+                op1=ALU.mult,
+            )
+
+        def residual_of_tile(t):
+            g, j = divmod(t, TILES_PER_GROUP)
+            gated_ps = psum.tile([P, HID], F32, name="gated_ps", tag="gated_ps")
+            for c in range(CHUNKS):
+                nc.tensor.transpose(gated_ps[:, c * P : (c + 1) * P], gated_t[g][:, c, j * P : (j + 1) * P], ident[:])
+            y[t] = work.tile([P, HID], F32, name="y", tag="y")
+            sum_y = stats.tile([P, 1], F32, name="sum_y", tag="sum_y")
+            nc.vector.scalar_tensor_tensor(
+                out=y[t][:],
+                in0=gated_ps[:],
+                scalar=1.0,
+                in1=hs_nat[g][:, j, :],
+                op0=ALU.mult,
+                op1=ALU.add,
+                accum_out=sum_y[:],
+            )
+            neg_mean[t] = stats.tile([P, 1], F32, name="neg_mean", tag="neg_mean")
+            nc.gpsimd.tensor_scalar(
+                out=neg_mean[t][:], in0=sum_y[:], scalar1=-1.0 / HID, scalar2=0.0, op0=ALU.mult, op1=ALU.add
+            )
+
+        def centre_tile(t):
+            squares = work.tile([P, HID], F32, name="squares", tag="squares", bufs=2)
+            sum_sq = stats.tile([P, 1], F32, name="sum_sq", tag="sum_sq")
+            nc.scalar.activation(
+                out=squares[:], in_=y[t][:], func=ACT.Square, bias=neg_mean[t][:], scale=1.0, accum_out=sum_sq[:]
+            )
+            centred[t] = work.tile([P, HID], F32, name="centred", tag="centred")
+            nc.vector.scalar_tensor_tensor(
+                out=centred[t][:],
+                in0=y[t][:],
+                scalar=neg_mean[t][:],
+                in1=gamma_rows[:],
+                op0=ALU.add,
+                op1=ALU.mult,
+            )
+            var_eps = stats.tile([P, 1], F32, name="var_eps", tag="var_eps")
+            nc.gpsimd.tensor_scalar(
+                out=var_eps[:], in0=sum_sq[:], scalar1=1.0 / HID, scalar2=LN_EPS, op0=ALU.mult, op1=ALU.add
+            )
+            rstd[t] = stats.tile([P, 1], F32, name="rstd", tag="rstd")
+            nc.gpsimd.tensor_tensor(out=rstd[t][:], in0=var_eps[:], in1=neg_half[:], op=ALU.pow)
+
+        def scale_tile(t):
+            g, j = divmod(t, TILES_PER_GROUP)
+            scaled = work.tile([P, HID], F32, name="scaled", tag="scaled")
+            nc.scalar.activation(out=scaled[:], in_=centred[t][:], func=ACT.Copy, scale=rstd[t][:])
+            result = work.tile([P, HID], F32, name="result", tag="result")
+            nc.gpsimd.tensor_tensor(out=result[:], in0=scaled[:], in1=beta_rows[:], op=ALU.add)
+            nc.sync.dma_start(out=out_dram[g][:, j, :], in_=result[:])
+
+        def runs(t):
+            return 0 <= t < N_TILES
+
+        for i in range(N_TILES + LAG_SCALE):
+            g_now, j_now = divmod(i, TILES_PER_GROUP)
+            if j_now == 0 and g_now + GROUPS_AHEAD < N_GROUPS:
+                load_group(g_now + GROUPS_AHEAD)
+            if runs(i - LAG_SCALE):
+                scale_tile(i - LAG_SCALE)
+            if runs(i - LAG_CENTRE):
+                centre_tile(i - LAG_CENTRE)
+            if runs(i - LAG_RESIDUAL):
+                residual_of_tile(i - LAG_RESIDUAL)
+            if runs(i - LAG_PRODUCTS):
+                products_of_chunk(i - LAG_PRODUCTS)
+            if runs(i - LAG_QUANTISE):
+                quantise_tile(i - LAG_QUANTISE)
+            if runs(i):
+                transpose_tile(i)

@@ -233,19 +233,20 @@ def tile_crossattentionlayer_pa_t_kernel(
         def runs(t):
             return 0 <= t < N_TILES
 
-        for i in range(N_TILES + LAG_SCALE):
-            g_now, j_now = divmod(i, TILES_PER_GROUP)
-            if j_now == 0 and g_now + GROUPS_AHEAD < N_GROUPS:
-                load_group(g_now + GROUPS_AHEAD)
-            if runs(i - LAG_SCALE):
-                scale_tile(i - LAG_SCALE)
-            if runs(i - LAG_CENTRE):
-                centre_tile(i - LAG_CENTRE)
-            if runs(i - LAG_RESIDUAL):
-                residual_of_tile(i - LAG_RESIDUAL)
-            if runs(i - LAG_PRODUCTS):
-                products_of_chunk(i - LAG_PRODUCTS)
-            if runs(i - LAG_QUANTISE):
-                quantise_tile(i - LAG_QUANTISE)
-            if runs(i):
-                transpose_tile(i)
+        with tc.manual_schedule():
+            for i in range(N_TILES + LAG_SCALE):
+                g_now, j_now = divmod(i, TILES_PER_GROUP)
+                if j_now == 0 and g_now + GROUPS_AHEAD < N_GROUPS:
+                    load_group(g_now + GROUPS_AHEAD)
+                if runs(i - LAG_SCALE):
+                    scale_tile(i - LAG_SCALE)
+                if runs(i - LAG_CENTRE):
+                    centre_tile(i - LAG_CENTRE)
+                if runs(i - LAG_RESIDUAL):
+                    residual_of_tile(i - LAG_RESIDUAL)
+                if runs(i - LAG_PRODUCTS):
+                    products_of_chunk(i - LAG_PRODUCTS)
+                if runs(i - LAG_QUANTISE):
+                    quantise_tile(i - LAG_QUANTISE)
+                if runs(i):
+                    transpose_tile(i)

@@ -27,8 +27,8 @@ CTX, HS = 0, 1
 LAG_QUANTISE = 2
 LAG_PRODUCTS = 7
 LAG_RESIDUAL = 12
-LAG_CENTRE = 14
-LAG_SCALE = 16
+LAG_CENTRE = 17
+LAG_SCALE = 22
 GROUPS_AHEAD = 2
 
 FLOPS = 2 * 2 * TOKENS * HID * HID
@@ -84,7 +84,7 @@ def tile_crossattentionlayer_pa_t_kernel(
 
         ident = consts.tile([P, P], F32, name="ident")
         make_identity(nc, ident[:])
-        neg_half = consts.tile([P, 1], F32, name="neg_half")
+        neg_half = consts.tile([P, TILES_PER_GROUP], F32, name="neg_half")
         nc.vector.memset(neg_half[:], -0.5)
 
         gamma_rows = consts.tile([P, HID], BF16, name="gamma_rows")
@@ -108,8 +108,10 @@ def tile_crossattentionlayer_pa_t_kernel(
         scales = {}
         gated_t = {}
         y = {}
-        neg_mean = {}
         centred = {}
+        sum_y = {}
+        neg_mean = {}
+        sum_sq = {}
         rstd = {}
 
         def transpose_tile(t):
@@ -184,8 +186,9 @@ def tile_crossattentionlayer_pa_t_kernel(
             gated_ps = psum.tile([P, HID], F32, name="gated_ps", tag="gated_ps")
             for c in range(CHUNKS):
                 nc.tensor.transpose(gated_ps[:, c * P : (c + 1) * P], gated_t[g][:, c, j * P : (j + 1) * P], ident[:])
-            y[t] = work.tile([P, HID], F32, name="y", tag="y")
-            sum_y = stats.tile([P, 1], F32, name="sum_y", tag="sum_y")
+            y[t] = work.tile([P, HID], F32, name="y", tag="y", bufs=8)
+            if j == 0:
+                sum_y[g] = stats.tile([P, TILES_PER_GROUP], F32, name="sum_y", tag="sum_y")
             nc.vector.scalar_tensor_tensor(
                 out=y[t][:],
                 in0=gated_ps[:],
@@ -193,60 +196,73 @@ def tile_crossattentionlayer_pa_t_kernel(
                 in1=hs_nat[g][:, j, :],
                 op0=ALU.mult,
                 op1=ALU.add,
-                accum_out=sum_y[:],
+                accum_out=sum_y[g][:, j : j + 1],
             )
-            neg_mean[t] = stats.tile([P, 1], F32, name="neg_mean", tag="neg_mean")
-            nc.gpsimd.tensor_scalar(
-                out=neg_mean[t][:], in0=sum_y[:], scalar1=-1.0 / HID, scalar2=0.0, op0=ALU.mult, op1=ALU.add
-            )
+            if j == TILES_PER_GROUP - 1:
+                neg_mean[g] = stats.tile([P, TILES_PER_GROUP], F32, name="neg_mean", tag="neg_mean")
+                nc.vector.tensor_scalar(
+                    out=neg_mean[g][:], in0=sum_y[g][:], scalar1=-1.0 / HID, scalar2=None, op0=ALU.mult
+                )
 
         def centre_tile(t):
+            g, j = divmod(t, TILES_PER_GROUP)
             squares = work.tile([P, HID], F32, name="squares", tag="squares", bufs=2)
-            sum_sq = stats.tile([P, 1], F32, name="sum_sq", tag="sum_sq")
+            if j == 0:
+                sum_sq[g] = stats.tile([P, TILES_PER_GROUP], F32, name="sum_sq", tag="sum_sq")
             nc.scalar.activation(
-                out=squares[:], in_=y[t][:], func=ACT.Square, bias=neg_mean[t][:], scale=1.0, accum_out=sum_sq[:]
+                out=squares[:],
+                in_=y[t][:],
+                func=ACT.Square,
+                bias=neg_mean[g][:, j : j + 1],
+                scale=1.0,
+                accum_out=sum_sq[g][:, j : j + 1],
             )
-            centred[t] = work.tile([P, HID], F32, name="centred", tag="centred")
+            centred[t] = work.tile([P, HID], F32, name="centred", tag="centred", bufs=8)
             nc.vector.scalar_tensor_tensor(
                 out=centred[t][:],
                 in0=y[t][:],
-                scalar=neg_mean[t][:],
+                scalar=neg_mean[g][:, j : j + 1],
                 in1=gamma_rows[:],
                 op0=ALU.add,
                 op1=ALU.mult,
             )
-            var_eps = stats.tile([P, 1], F32, name="var_eps", tag="var_eps")
-            nc.gpsimd.tensor_scalar(
-                out=var_eps[:], in0=sum_sq[:], scalar1=1.0 / HID, scalar2=LN_EPS, op0=ALU.mult, op1=ALU.add
-            )
-            rstd[t] = stats.tile([P, 1], F32, name="rstd", tag="rstd")
-            nc.gpsimd.tensor_tensor(out=rstd[t][:], in0=var_eps[:], in1=neg_half[:], op=ALU.pow)
+            if j == TILES_PER_GROUP - 1:
+                var_eps = stats.tile([P, TILES_PER_GROUP], F32, name="var_eps", tag="var_eps")
+                nc.vector.tensor_scalar(
+                    out=var_eps[:], in0=sum_sq[g][:], scalar1=1.0 / HID, scalar2=LN_EPS, op0=ALU.mult, op1=ALU.add
+                )
+                rstd[g] = stats.tile([P, TILES_PER_GROUP], F32, name="rstd", tag="rstd")
+                nc.gpsimd.tensor_tensor(out=rstd[g][:], in0=var_eps[:], in1=neg_half[:], op=ALU.pow)
 
         def scale_tile(t):
             g, j = divmod(t, TILES_PER_GROUP)
-            scaled = work.tile([P, HID], F32, name="scaled", tag="scaled")
-            nc.scalar.activation(out=scaled[:], in_=centred[t][:], func=ACT.Copy, scale=rstd[t][:])
             result = work.tile([P, HID], F32, name="result", tag="result")
-            nc.gpsimd.tensor_tensor(out=result[:], in0=scaled[:], in1=beta_rows[:], op=ALU.add)
+            nc.vector.scalar_tensor_tensor(
+                out=result[:],
+                in0=centred[t][:],
+                scalar=rstd[g][:, j : j + 1],
+                in1=beta_rows[:],
+                op0=ALU.mult,
+                op1=ALU.add,
+            )
             nc.sync.dma_start(out=out_dram[g][:, j, :], in_=result[:])
 
         def runs(t):
             return 0 <= t < N_TILES
 
-        with tc.manual_schedule():
-            for i in range(N_TILES + LAG_SCALE):
-                g_now, j_now = divmod(i, TILES_PER_GROUP)
-                if j_now == 0 and g_now + GROUPS_AHEAD < N_GROUPS:
-                    load_group(g_now + GROUPS_AHEAD)
-                if runs(i - LAG_SCALE):
-                    scale_tile(i - LAG_SCALE)
-                if runs(i - LAG_CENTRE):
-                    centre_tile(i - LAG_CENTRE)
-                if runs(i - LAG_RESIDUAL):
-                    residual_of_tile(i - LAG_RESIDUAL)
-                if runs(i - LAG_PRODUCTS):
-                    products_of_chunk(i - LAG_PRODUCTS)
-                if runs(i - LAG_QUANTISE):
-                    quantise_tile(i - LAG_QUANTISE)
-                if runs(i):
-                    transpose_tile(i)
+        for i in range(N_TILES + LAG_SCALE):
+            g_now, j_now = divmod(i, TILES_PER_GROUP)
+            if j_now == 0 and g_now + GROUPS_AHEAD < N_GROUPS:
+                load_group(g_now + GROUPS_AHEAD)
+            if runs(i - LAG_SCALE):
+                scale_tile(i - LAG_SCALE)
+            if runs(i - LAG_CENTRE):
+                centre_tile(i - LAG_CENTRE)
+            if runs(i - LAG_RESIDUAL):
+                residual_of_tile(i - LAG_RESIDUAL)
+            if runs(i - LAG_PRODUCTS):
+                products_of_chunk(i - LAG_PRODUCTS)
+            if runs(i - LAG_QUANTISE):
+                quantise_tile(i - LAG_QUANTISE)
+            if runs(i):
+                transpose_tile(i)

@@ -49,6 +49,7 @@ def tile_crossattentionlayer_pa_t_kernel(
         work = stack.enter_context(tc.tile_pool(name="work", bufs=4))
         stats = stack.enter_context(tc.tile_pool(name="stats", bufs=6))
         psum = stack.enter_context(tc.psum_pool(name="psum", bufs=2))
+        psum_keep = stack.enter_context(tc.psum_pool(name="psum_keep", bufs=1))
 
         def quantise_weight(w, label):
             raw = consts.tile([P, PACK, HID], BF16, name=label + "_raw")
@@ -87,10 +88,15 @@ def tile_crossattentionlayer_pa_t_kernel(
         neg_half = consts.tile([P, TILES_PER_GROUP], F32, name="neg_half")
         nc.vector.memset(neg_half[:], -0.5)
 
-        gamma_rows = consts.tile([P, HID], BF16, name="gamma_rows")
-        nc.scalar.dma_start(out=gamma_rows[:], in_=ln_gamma.partition_broadcast(P))
         beta_rows = consts.tile([P, HID], BF16, name="beta_rows")
         nc.scalar.dma_start(out=beta_rows[:], in_=ln_beta.partition_broadcast(P))
+        ones = consts.tile([P, P], BF16, name="ones")
+        nc.vector.memset(ones[:], 1.0)
+        gamma_row0 = consts.tile([P, HID], BF16, name="gamma_row0")
+        nc.vector.memset(gamma_row0[:], 0.0)
+        nc.scalar.dma_start(out=gamma_row0[0:1, :], in_=ln_gamma.rearrange("(o f) -> o f", o=1))
+        gamma_rows = psum_keep.tile([P, HID], F32, name="gamma_rows")
+        nc.tensor.matmul(out=gamma_rows[:], lhsT=ones[:], rhs=gamma_row0[:], start=True, stop=True)
 
         bias_rows = consts.tile([P, P], BF16, name="bias_rows")
         nc.vector.memset(bias_rows[:], 0.0)
@@ -130,17 +136,14 @@ def tile_crossattentionlayer_pa_t_kernel(
                 in_=words_ps[:].rearrange("p o u r -> p o r u"),
             )
 
-        def quantise_tile(t):
-            g, j = divmod(t, TILES_PER_GROUP)
-            if j == 0:
-                codes[g] = work.tile([P, 2, GROUP], U32, name="codes", tag="codes", bufs=3, align_bytes=64)
-                scales[g] = work.tile([P, 2, GROUP], U8, name="scales", tag="scales", bufs=3, align_bytes=64)
-            cols = slice(j * P, (j + 1) * P)
+        def quantise_group(g):
+            codes[g] = work.tile([P, 2, GROUP], U32, name="codes", tag="codes", bufs=3, align_bytes=64)
+            scales[g] = work.tile([P, 2, GROUP], U8, name="scales", tag="scales", bufs=3, align_bytes=64)
             for operand in (CTX, HS):
                 nc.vector.quantize_mx(
-                    out=codes[g][:, operand, cols].bitcast(FP8X4),
-                    scales=scales[g][:, operand, cols],
-                    in_=grouped[g][:, operand, cols, :].rearrange("p r t -> p (r t)"),
+                    out=codes[g][:, operand, :].bitcast(FP8X4),
+                    scales=scales[g][:, operand, :],
+                    in_=grouped[g][:, operand, :, :].rearrange("p r t -> p (r t)"),
                 )
 
         def products_of_chunk(s):
@@ -158,7 +161,7 @@ def tile_crossattentionlayer_pa_t_kernel(
                 start=True,
                 stop=True,
             )
-            gate_ps = psum.tile([P, GROUP], F32, name="gate_ps", tag="gate_ps")
+            gate_ps = psum.tile([P, GROUP], F32, name="gate_ps", tag="gate_ps", bufs=1)
             nc.tensor.matmul_mx(
                 out=gate_ps[:],
                 lhsT=wg_codes[:, feats].bitcast(FP8X4),
@@ -236,15 +239,10 @@ def tile_crossattentionlayer_pa_t_kernel(
 
         def scale_tile(t):
             g, j = divmod(t, TILES_PER_GROUP)
+            scaled = work.tile([P, HID], F32, name="scaled", tag="scaled")
+            nc.scalar.activation(out=scaled[:], in_=centred[t][:], func=ACT.Copy, scale=rstd[g][:, j : j + 1])
             result = work.tile([P, HID], F32, name="result", tag="result")
-            nc.vector.scalar_tensor_tensor(
-                out=result[:],
-                in0=centred[t][:],
-                scalar=rstd[g][:, j : j + 1],
-                in1=beta_rows[:],
-                op0=ALU.mult,
-                op1=ALU.add,
-            )
+            nc.gpsimd.tensor_tensor(out=result[:], in0=scaled[:], in1=beta_rows[:], op=ALU.add)
             nc.sync.dma_start(out=out_dram[g][:, j, :], in_=result[:])
 
         def runs(t):
@@ -262,7 +260,7 @@ def tile_crossattentionlayer_pa_t_kernel(
                 residual_of_tile(i - LAG_RESIDUAL)
             if runs(i - LAG_PRODUCTS):
                 products_of_chunk(i - LAG_PRODUCTS)
-            if runs(i - LAG_QUANTISE):
-                quantise_tile(i - LAG_QUANTISE)
+            if runs(i - LAG_QUANTISE) and (i - LAG_QUANTISE) % TILES_PER_GROUP == TILES_PER_GROUP - 1:
+                quantise_group((i - LAG_QUANTISE) // TILES_PER_GROUP)
             if runs(i):
                 transpose_tile(i)

@@ -139,12 +139,11 @@ def tile_crossattentionlayer_pa_t_kernel(
         def quantise_group(g):
             codes[g] = work.tile([P, 2, GROUP], U32, name="codes", tag="codes", bufs=3, align_bytes=64)
             scales[g] = work.tile([P, 2, GROUP], U8, name="scales", tag="scales", bufs=3, align_bytes=64)
-            for operand in (CTX, HS):
-                nc.vector.quantize_mx(
-                    out=codes[g][:, operand, :].bitcast(FP8X4),
-                    scales=scales[g][:, operand, :],
-                    in_=grouped[g][:, operand, :, :].rearrange("p r t -> p (r t)"),
-                )
+            nc.vector.quantize_mx(
+                out=codes[g][:].rearrange("p o r -> p (o r)").bitcast(FP8X4),
+                scales=scales[g][:].rearrange("p o r -> p (o r)"),
+                in_=grouped[g][:].rearrange("p o r t -> p (o r t)"),
+            )
 
         def products_of_chunk(s):
             g, c = divmod(s, CHUNKS)
@@ -203,7 +202,7 @@ def tile_crossattentionlayer_pa_t_kernel(
             )
             if j == TILES_PER_GROUP - 1:
                 neg_mean[g] = stats.tile([P, TILES_PER_GROUP], F32, name="neg_mean", tag="neg_mean")
-                nc.vector.tensor_scalar(
+                nc.gpsimd.tensor_scalar(
                     out=neg_mean[g][:], in0=sum_y[g][:], scalar1=-1.0 / HID, scalar2=None, op0=ALU.mult
                 )
 
@@ -231,7 +230,7 @@ def tile_crossattentionlayer_pa_t_kernel(
             )
             if j == TILES_PER_GROUP - 1:
                 var_eps = stats.tile([P, TILES_PER_GROUP], F32, name="var_eps", tag="var_eps")
-                nc.vector.tensor_scalar(
+                nc.gpsimd.tensor_scalar(
                     out=var_eps[:], in0=sum_sq[g][:], scalar1=1.0 / HID, scalar2=LN_EPS, op0=ALU.mult, op1=ALU.add
                 )
                 rstd[g] = stats.tile([P, TILES_PER_GROUP], F32, name="rstd", tag="rstd")

@@ -85,6 +85,8 @@ def tile_crossattentionlayer_pa_t_kernel(
 
         ident = consts.tile([P, P], F32, name="ident")
         make_identity(nc, ident[:])
+        ident_bf16 = consts.tile([P, P], BF16, name="ident_bf16")
+        make_identity(nc, ident_bf16[:])
         neg_half = consts.tile([P, TILES_PER_GROUP], F32, name="neg_half")
         nc.vector.memset(neg_half[:], -0.5)
 
@@ -185,21 +187,36 @@ def tile_crossattentionlayer_pa_t_kernel(
 
         def residual_of_tile(t):
             g, j = divmod(t, TILES_PER_GROUP)
+            on_vector = j == TILES_PER_GROUP - 1
             gated_ps = psum.tile([P, HID], F32, name="gated_ps", tag="gated_ps")
+            if not on_vector:
+                nc.tensor.matmul(out=gated_ps[:], lhsT=ident_bf16[:], rhs=hs_nat[g][:, j, :], start=True, stop=False)
             for c in range(CHUNKS):
-                nc.tensor.transpose(gated_ps[:, c * P : (c + 1) * P], gated_t[g][:, c, j * P : (j + 1) * P], ident[:])
+                nc.tensor.matmul(
+                    out=gated_ps[:, c * P : (c + 1) * P],
+                    lhsT=gated_t[g][:, c, j * P : (j + 1) * P],
+                    rhs=ident[:],
+                    is_transpose=True,
+                    start=on_vector,
+                    stop=on_vector or c == CHUNKS - 1,
+                )
             y[t] = work.tile([P, HID], F32, name="y", tag="y", bufs=8)
             if j == 0:
                 sum_y[g] = stats.tile([P, TILES_PER_GROUP], F32, name="sum_y", tag="sum_y")
-            nc.vector.scalar_tensor_tensor(
-                out=y[t][:],
-                in0=gated_ps[:],
-                scalar=1.0,
-                in1=hs_nat[g][:, j, :],
-                op0=ALU.mult,
-                op1=ALU.add,
-                accum_out=sum_y[g][:, j : j + 1],
-            )
+            if on_vector:
+                nc.vector.scalar_tensor_tensor(
+                    out=y[t][:],
+                    in0=gated_ps[:],
+                    scalar=1.0,
+                    in1=hs_nat[g][:, j, :],
+                    op0=ALU.mult,
+                    op1=ALU.add,
+                    accum_out=sum_y[g][:, j : j + 1],
+                )
+            else:
+                nc.scalar.activation(
+                    out=y[t][:], in_=gated_ps[:], func=ACT.Copy, scale=1.0, accum_out=sum_y[g][:, j : j + 1]
+                )
             if j == TILES_PER_GROUP - 1:
                 neg_mean[g] = stats.tile([P, TILES_PER_GROUP], F32, name="neg_mean", tag="neg_mean")
                 nc.gpsimd.tensor_scalar(
@@ -238,10 +255,15 @@ def tile_crossattentionlayer_pa_t_kernel(
 
         def scale_tile(t):
             g, j = divmod(t, TILES_PER_GROUP)
-            scaled = work.tile([P, HID], F32, name="scaled", tag="scaled")
-            nc.scalar.activation(out=scaled[:], in_=centred[t][:], func=ACT.Copy, scale=rstd[g][:, j : j + 1])
             result = work.tile([P, HID], F32, name="result", tag="result")
-            nc.gpsimd.tensor_tensor(out=result[:], in0=scaled[:], in1=beta_rows[:], op=ALU.add)
+            nc.vector.scalar_tensor_tensor(
+                out=result[:],
+                in0=centred[t][:],
+                scalar=rstd[g][:, j : j + 1],
+                in1=beta_rows[:],
+                op0=ALU.mult,
+                op1=ALU.add,
+            )
             nc.sync.dma_start(out=out_dram[g][:, j, :], in_=result[:])
 
         def runs(t):

@@ -24,11 +24,16 @@ N_GROUPS = TOKENS // GROUP
 N_TILES = TOKENS // P
 CTX, HS = 0, 1
 
+LAG_TRANSPOSE = 0
+LAG_COPY = 1
 LAG_QUANTISE = 2
 LAG_PRODUCTS = 7
-LAG_RESIDUAL = 12
-LAG_CENTRE = 17
-LAG_SCALE = 22
+LAG_GATE = 8
+LAG_GATED = 9
+LAG_RESIDUAL = 13
+LAG_Y = 14
+LAG_CENTRE = 18
+LAG_SCALE = 23
 GROUPS_AHEAD = 2
 
 FLOPS = 2 * 2 * TOKENS * HID * HID
@@ -49,7 +54,6 @@ def tile_crossattentionlayer_pa_t_kernel(
         work = stack.enter_context(tc.tile_pool(name="work", bufs=4))
         stats = stack.enter_context(tc.tile_pool(name="stats", bufs=6))
         psum = stack.enter_context(tc.psum_pool(name="psum", bufs=2))
-        psum_keep = stack.enter_context(tc.psum_pool(name="psum_keep", bufs=1))
 
         def quantise_weight(w, label):
             raw = consts.tile([P, PACK, HID], BF16, name=label + "_raw")
@@ -92,13 +96,8 @@ def tile_crossattentionlayer_pa_t_kernel(
 
         beta_rows = consts.tile([P, HID], BF16, name="beta_rows")
         nc.scalar.dma_start(out=beta_rows[:], in_=ln_beta.partition_broadcast(P))
-        ones = consts.tile([P, P], BF16, name="ones")
-        nc.vector.memset(ones[:], 1.0)
-        gamma_row0 = consts.tile([P, HID], BF16, name="gamma_row0")
-        nc.vector.memset(gamma_row0[:], 0.0)
-        nc.scalar.dma_start(out=gamma_row0[0:1, :], in_=ln_gamma.rearrange("(o f) -> o f", o=1))
-        gamma_rows = psum_keep.tile([P, HID], F32, name="gamma_rows")
-        nc.tensor.matmul(out=gamma_rows[:], lhsT=ones[:], rhs=gamma_row0[:], start=True, stop=True)
+        gamma_rows = consts.tile([P, HID], BF16, name="gamma_rows")
+        nc.scalar.dma_start(out=gamma_rows[:], in_=ln_gamma.partition_broadcast(P))
 
         bias_rows = consts.tile([P, P], BF16, name="bias_rows")
         nc.vector.memset(bias_rows[:], 0.0)
@@ -122,23 +121,35 @@ def tile_crossattentionlayer_pa_t_kernel(
         sum_sq = {}
         rstd = {}
 
+        words_ps = {}
+        attn_ps = {}
+        gate_ps = {}
+        gate = {}
+        y_ps = {}
+
         def transpose_tile(t):
+            g, j = divmod(t, TILES_PER_GROUP)
+            words_ps[t] = psum.tile([P, 2, 2, P], F32, name="words_ps", tag="words_ps")
+            for operand, nat in ((CTX, ctx_nat[g]), (HS, hs_nat[g])):
+                words = nat[:].bitcast(F32)
+                for u in range(2):
+                    nc.tensor.transpose(words_ps[t][:, operand, u, :], words[:, j, u * P : (u + 1) * P], ident[:])
+
+        def copy_tile(t):
             g, j = divmod(t, TILES_PER_GROUP)
             if j == 0:
                 grouped[g] = work.tile(
                     [P, 2, GROUP, PACK], BF16, name="grouped", tag="grouped", bufs=2, align_bytes=64
                 )
-            words_ps = psum.tile([P, 2, 2, P], F32, name="words_ps", tag="words_ps")
-            for operand, nat in ((CTX, ctx_nat[g]), (HS, hs_nat[g])):
-                words = nat[:].bitcast(F32)
-                for u in range(2):
-                    nc.tensor.transpose(words_ps[:, operand, u, :], words[:, j, u * P : (u + 1) * P], ident[:])
             nc.scalar.copy(
                 out=grouped[g][:].bitcast(F32)[:, :, j * P : (j + 1) * P, :],
-                in_=words_ps[:].rearrange("p o u r -> p o r u"),
+                in_=words_ps[t][:].rearrange("p o u r -> p o r u"),
             )
 
-        def quantise_group(g):
+        def quantise_tile(t):
+            g, j = divmod(t, TILES_PER_GROUP)
+            if j < TILES_PER_GROUP - 1:
+                return
             codes[g] = work.tile([P, 2, GROUP], U32, name="codes", tag="codes", bufs=3, align_bytes=64)
             scales[g] = work.tile([P, 2, GROUP], U8, name="scales", tag="scales", bufs=3, align_bytes=64)
             nc.vector.quantize_mx(
@@ -149,64 +160,75 @@ def tile_crossattentionlayer_pa_t_kernel(
 
         def products_of_chunk(s):
             g, c = divmod(s, CHUNKS)
+            feats = slice(c * P, (c + 1) * P)
+            gate_ps[s] = psum.tile([P, GROUP], F32, name="gate_ps", tag="gate_ps")
+            attn_ps[s] = psum.tile([P, GROUP], F32, name="attn_ps", tag="attn_ps")
+            for product, w_codes, w_scales, operand in (
+                (gate_ps[s], wg_codes, wg_scales, HS),
+                (attn_ps[s], wo_codes, wo_scales, CTX),
+            ):
+                nc.tensor.matmul_mx(
+                    out=product[:],
+                    lhsT=w_codes[:, feats].bitcast(FP8X4),
+                    lhsT_scale=w_scales[:, feats],
+                    rhs=codes[g][:, operand, :].bitcast(FP8X4),
+                    rhs_scale=scales[g][:, operand, :],
+                    start=True,
+                    stop=True,
+                )
+
+        def gate_of_chunk(s):
+            g, c = divmod(s, CHUNKS)
+            gate[s] = work.tile([P, GROUP], F32, name="gate", tag="gate")
+            nc.scalar.activation(
+                out=gate[s][:],
+                in_=gate_ps[s][:],
+                func=ACT.Sigmoid,
+                bias=bias_cols[:, CHUNKS + c : CHUNKS + c + 1],
+                scale=1.0,
+            )
+
+        def gated_chunk(s):
+            g, c = divmod(s, CHUNKS)
             if c == 0:
                 gated_t[g] = work.tile([P, CHUNKS, GROUP], F32, name="gated_t", tag="gated_t", bufs=3)
-            feats = slice(c * P, (c + 1) * P)
-            attn_ps = psum.tile([P, GROUP], F32, name="attn_ps", tag="attn_ps")
-            nc.tensor.matmul_mx(
-                out=attn_ps[:],
-                lhsT=wo_codes[:, feats].bitcast(FP8X4),
-                lhsT_scale=wo_scales[:, feats],
-                rhs=codes[g][:, CTX, :].bitcast(FP8X4),
-                rhs_scale=scales[g][:, CTX, :],
-                start=True,
-                stop=True,
-            )
-            gate_ps = psum.tile([P, GROUP], F32, name="gate_ps", tag="gate_ps", bufs=1)
-            nc.tensor.matmul_mx(
-                out=gate_ps[:],
-                lhsT=wg_codes[:, feats].bitcast(FP8X4),
-                lhsT_scale=wg_scales[:, feats],
-                rhs=codes[g][:, HS, :].bitcast(FP8X4),
-                rhs_scale=scales[g][:, HS, :],
-                start=True,
-                stop=True,
-            )
-            gate = work.tile([P, GROUP], F32, name="gate", tag="gate")
-            nc.scalar.activation(
-                out=gate[:], in_=gate_ps[:], func=ACT.Sigmoid, bias=bias_cols[:, CHUNKS + c : CHUNKS + c + 1], scale=1.0
-            )
             nc.vector.scalar_tensor_tensor(
                 out=gated_t[g][:, c, :],
-                in0=attn_ps[:],
+                in0=attn_ps[s][:],
                 scalar=bias_cols[:, c : c + 1],
-                in1=gate[:],
+                in1=gate[s][:],
                 op0=ALU.add,
                 op1=ALU.mult,
             )
 
+        def adds_on_vector(t):
+            return t % TILES_PER_GROUP == TILES_PER_GROUP - 1
+
         def residual_of_tile(t):
             g, j = divmod(t, TILES_PER_GROUP)
-            on_vector = j == TILES_PER_GROUP - 1
-            gated_ps = psum.tile([P, HID], F32, name="gated_ps", tag="gated_ps")
-            if not on_vector:
-                nc.tensor.matmul(out=gated_ps[:], lhsT=ident_bf16[:], rhs=hs_nat[g][:, j, :], start=True, stop=False)
+            y_ps[t] = psum.tile([P, HID], F32, name="y_ps", tag="y_ps")
+            alone = adds_on_vector(t)
+            if not alone:
+                nc.tensor.matmul(out=y_ps[t][:], lhsT=ident_bf16[:], rhs=hs_nat[g][:, j, :], start=True, stop=False)
             for c in range(CHUNKS):
                 nc.tensor.matmul(
-                    out=gated_ps[:, c * P : (c + 1) * P],
+                    out=y_ps[t][:, c * P : (c + 1) * P],
                     lhsT=gated_t[g][:, c, j * P : (j + 1) * P],
                     rhs=ident[:],
                     is_transpose=True,
-                    start=on_vector,
-                    stop=on_vector or c == CHUNKS - 1,
+                    start=alone,
+                    stop=alone or c == CHUNKS - 1,
                 )
-            y[t] = work.tile([P, HID], F32, name="y", tag="y", bufs=8)
+
+        def y_of_tile(t):
+            g, j = divmod(t, TILES_PER_GROUP)
+            y[t] = work.tile([P, HID], F32, name="y", tag="y", bufs=10)
             if j == 0:
                 sum_y[g] = stats.tile([P, TILES_PER_GROUP], F32, name="sum_y", tag="sum_y")
-            if on_vector:
+            if adds_on_vector(t):
                 nc.vector.scalar_tensor_tensor(
                     out=y[t][:],
-                    in0=gated_ps[:],
+                    in0=y_ps[t][:],
                     scalar=1.0,
                     in1=hs_nat[g][:, j, :],
                     op0=ALU.mult,
@@ -215,7 +237,7 @@ def tile_crossattentionlayer_pa_t_kernel(
                 )
             else:
                 nc.scalar.activation(
-                    out=y[t][:], in_=gated_ps[:], func=ACT.Copy, scale=1.0, accum_out=sum_y[g][:, j : j + 1]
+                    out=y[t][:], in_=y_ps[t][:], func=ACT.Copy, scale=1.0, accum_out=sum_y[g][:, j : j + 1]
                 )
             if j == TILES_PER_GROUP - 1:
                 neg_mean[g] = stats.tile([P, TILES_PER_GROUP], F32, name="neg_mean", tag="neg_mean")
@@ -223,7 +245,7 @@ def tile_crossattentionlayer_pa_t_kernel(
                     out=neg_mean[g][:], in0=sum_y[g][:], scalar1=-1.0 / HID, scalar2=None, op0=ALU.mult
                 )
 
-        def centre_tile(t):
+        def variance_of_tile(t):
             g, j = divmod(t, TILES_PER_GROUP)
             squares = work.tile([P, HID], F32, name="squares", tag="squares", bufs=2)
             if j == 0:
@@ -236,6 +258,16 @@ def tile_crossattentionlayer_pa_t_kernel(
                 scale=1.0,
                 accum_out=sum_sq[g][:, j : j + 1],
             )
+            if j == TILES_PER_GROUP - 1:
+                var_eps = stats.tile([P, TILES_PER_GROUP], F32, name="var_eps", tag="var_eps")
+                nc.gpsimd.tensor_scalar(
+                    out=var_eps[:], in0=sum_sq[g][:], scalar1=1.0 / HID, scalar2=LN_EPS, op0=ALU.mult, op1=ALU.add
+                )
+                rstd[g] = stats.tile([P, TILES_PER_GROUP], F32, name="rstd", tag="rstd")
+                nc.gpsimd.tensor_tensor(out=rstd[g][:], in0=var_eps[:], in1=neg_half[:], op=ALU.pow)
+
+        def centre_tile(t):
+            g, j = divmod(t, TILES_PER_GROUP)
             centred[t] = work.tile([P, HID], F32, name="centred", tag="centred", bufs=8)
             nc.vector.scalar_tensor_tensor(
                 out=centred[t][:],
@@ -245,13 +277,6 @@ def tile_crossattentionlayer_pa_t_kernel(
                 op0=ALU.add,
                 op1=ALU.mult,
             )
-            if j == TILES_PER_GROUP - 1:
-                var_eps = stats.tile([P, TILES_PER_GROUP], F32, name="var_eps", tag="var_eps")
-                nc.gpsimd.tensor_scalar(
-                    out=var_eps[:], in0=sum_sq[g][:], scalar1=1.0 / HID, scalar2=LN_EPS, op0=ALU.mult, op1=ALU.add
-                )
-                rstd[g] = stats.tile([P, TILES_PER_GROUP], F32, name="rstd", tag="rstd")
-                nc.gpsimd.tensor_tensor(out=rstd[g][:], in0=var_eps[:], in1=neg_half[:], op=ALU.pow)
 
         def scale_tile(t):
             g, j = divmod(t, TILES_PER_GROUP)
@@ -266,22 +291,24 @@ def tile_crossattentionlayer_pa_t_kernel(
             )
             nc.sync.dma_start(out=out_dram[g][:, j, :], in_=result[:])
 
-        def runs(t):
-            return 0 <= t < N_TILES
-
-        for i in range(N_TILES + LAG_SCALE):
-            g_now, j_now = divmod(i, TILES_PER_GROUP)
-            if j_now == 0 and g_now + GROUPS_AHEAD < N_GROUPS:
-                load_group(g_now + GROUPS_AHEAD)
-            if runs(i - LAG_SCALE):
-                scale_tile(i - LAG_SCALE)
-            if runs(i - LAG_CENTRE):
-                centre_tile(i - LAG_CENTRE)
-            if runs(i - LAG_RESIDUAL):
-                residual_of_tile(i - LAG_RESIDUAL)
-            if runs(i - LAG_PRODUCTS):
-                products_of_chunk(i - LAG_PRODUCTS)
-            if runs(i - LAG_QUANTISE) and (i - LAG_QUANTISE) % TILES_PER_GROUP == TILES_PER_GROUP - 1:
-                quantise_group((i - LAG_QUANTISE) // TILES_PER_GROUP)
-            if runs(i):
-                transpose_tile(i)
+        stages = (
+            (residual_of_tile, LAG_RESIDUAL),
+            (transpose_tile, LAG_TRANSPOSE),
+            (products_of_chunk, LAG_PRODUCTS),
+            (y_of_tile, LAG_Y),
+            (gate_of_chunk, LAG_GATE),
+            (variance_of_tile, LAG_CENTRE),
+            (copy_tile, LAG_COPY),
+            (gated_chunk, LAG_GATED),
+            (centre_tile, LAG_CENTRE),
+            (scale_tile, LAG_SCALE),
+            (quantise_tile, LAG_QUANTISE),
+        )
+        with tc.manual_schedule():
+            for i in range(N_TILES + LAG_SCALE):
+                g_now, j_now = divmod(i, TILES_PER_GROUP)
+                if j_now == 0 and g_now + GROUPS_AHEAD < N_GROUPS:
+                    load_group(g_now + GROUPS_AHEAD)
+                for stage, lag in stages:
+                    if 0 <= i - lag < N_TILES:
+                        stage(i - lag)

@@ -54,6 +54,7 @@ def tile_crossattentionlayer_pa_t_kernel(
         work = stack.enter_context(tc.tile_pool(name="work", bufs=4))
         stats = stack.enter_context(tc.tile_pool(name="stats", bufs=6))
         psum = stack.enter_context(tc.psum_pool(name="psum", bufs=2))
+        psum_keep = stack.enter_context(tc.psum_pool(name="psum_keep", bufs=1))
 
         def quantise_weight(w, label):
             raw = consts.tile([P, PACK, HID], BF16, name=label + "_raw")
@@ -72,9 +73,6 @@ def tile_crossattentionlayer_pa_t_kernel(
             )
             return w_codes, w_scales
 
-        wo_codes, wo_scales = quantise_weight(Wo, "wo")
-        wg_codes, wg_scales = quantise_weight(Wg, "wg")
-
         ctx_nat = {}
         hs_nat = {}
 
@@ -84,9 +82,16 @@ def tile_crossattentionlayer_pa_t_kernel(
             hs_nat[g] = loads.tile([P, TILES_PER_GROUP, HID], BF16, name="hs_nat", tag="hs_nat", bufs=7)
             nc.sync.dma_start(out=hs_nat[g][:], in_=hs_dram[g])
 
-        for g in range(GROUPS_AHEAD):
+        load_group(0)
+        wg_codes, wg_scales = quantise_weight(Wg, "wg")
+        wo_codes, wo_scales = quantise_weight(Wo, "wo")
+        for g in range(1, GROUPS_AHEAD):
             load_group(g)
 
+        table_in = consts.tile([P, 1], F32, name="table_in")
+        nc.vector.memset(table_in[:], 0.0)
+        table_out = consts.tile([P, 1], F32, name="table_out")
+        nc.scalar.activation(out=table_out[:], in_=table_in[:], func=ACT.Sigmoid, bias=0.0, scale=1.0)
         ident = consts.tile([P, P], F32, name="ident")
         make_identity(nc, ident[:])
         ident_bf16 = consts.tile([P, P], BF16, name="ident_bf16")
@@ -94,10 +99,15 @@ def tile_crossattentionlayer_pa_t_kernel(
         neg_half = consts.tile([P, TILES_PER_GROUP], F32, name="neg_half")
         nc.vector.memset(neg_half[:], -0.5)
 
-        beta_rows = consts.tile([P, HID], BF16, name="beta_rows")
-        nc.scalar.dma_start(out=beta_rows[:], in_=ln_beta.partition_broadcast(P))
-        gamma_rows = consts.tile([P, HID], BF16, name="gamma_rows")
-        nc.scalar.dma_start(out=gamma_rows[:], in_=ln_gamma.partition_broadcast(P))
+        ones = consts.tile([P, P], BF16, name="ones")
+        nc.vector.memset(ones[:], 1.0)
+        vector_row0 = consts.tile([P, 2, HID], BF16, name="vector_row0")
+        nc.vector.memset(vector_row0[:], 0.0)
+        nc.scalar.dma_start(out=vector_row0[0:1, 0, :], in_=ln_gamma.rearrange("(o f) -> o f", o=1))
+        nc.scalar.dma_start(out=vector_row0[0:1, 1, :], in_=ln_beta.rearrange("(o f) -> o f", o=1))
+        vector_rows = psum_keep.tile([P, 2, HID], BF16, name="vector_rows")
+        gamma_rows = vector_rows[:, 0, :]
+        beta_rows = vector_rows[:, 1, :]
 
         bias_rows = consts.tile([P, P], BF16, name="bias_rows")
         nc.vector.memset(bias_rows[:], 0.0)
@@ -105,10 +115,16 @@ def tile_crossattentionlayer_pa_t_kernel(
         nc.scalar.dma_start(out=bias_rows[CHUNKS : 2 * CHUNKS, :], in_=bg.rearrange("(c f) -> c f", f=P))
         bias_rows_f32 = consts.tile([P, P], F32, name="bias_rows_f32")
         nc.vector.tensor_copy(out=bias_rows_f32[:], in_=bias_rows[:])
-        bias_ps = psum.tile([P, P], F32, name="bias_ps", tag="words_ps")
-        nc.tensor.transpose(bias_ps[:], bias_rows_f32[:], ident[:])
         bias_cols = consts.tile([P, 2 * CHUNKS], F32, name="bias_cols")
-        nc.vector.tensor_copy(out=bias_cols[:], in_=bias_ps[:, 0 : 2 * CHUNKS])
+
+        def constants_on_tensor():
+            for v in range(2):
+                nc.tensor.matmul(
+                    out=vector_rows[:, v, :], lhsT=ones[:], rhs=vector_row0[:, v, :], start=True, stop=True
+                )
+            bias_ps = psum.tile([P, P], F32, name="bias_ps", tag="y_ps")
+            nc.tensor.transpose(bias_ps[:], bias_rows_f32[:], ident[:])
+            nc.vector.tensor_copy(out=bias_cols[:], in_=bias_ps[:, 0 : 2 * CHUNKS])
 
         grouped = {}
         codes = {}
@@ -161,7 +177,7 @@ def tile_crossattentionlayer_pa_t_kernel(
         def products_of_chunk(s):
             g, c = divmod(s, CHUNKS)
             feats = slice(c * P, (c + 1) * P)
-            gate_ps[s] = psum.tile([P, GROUP], F32, name="gate_ps", tag="gate_ps")
+            gate_ps[s] = psum.tile([P, GROUP], F32, name="gate_ps", tag="gate_ps", bufs=1)
             attn_ps[s] = psum.tile([P, GROUP], F32, name="attn_ps", tag="attn_ps")
             for product, w_codes, w_scales, operand in (
                 (gate_ps[s], wg_codes, wg_scales, HS),
@@ -273,7 +289,7 @@ def tile_crossattentionlayer_pa_t_kernel(
                 out=centred[t][:],
                 in0=y[t][:],
                 scalar=neg_mean[g][:, j : j + 1],
-                in1=gamma_rows[:],
+                in1=gamma_rows,
                 op0=ALU.add,
                 op1=ALU.mult,
             )
@@ -285,7 +301,7 @@ def tile_crossattentionlayer_pa_t_kernel(
                 out=result[:],
                 in0=centred[t][:],
                 scalar=rstd[g][:, j : j + 1],
-                in1=beta_rows[:],
+                in1=beta_rows,
                 op0=ALU.mult,
                 op1=ALU.add,
             )
@@ -309,6 +325,8 @@ def tile_crossattentionlayer_pa_t_kernel(
                 g_now, j_now = divmod(i, TILES_PER_GROUP)
                 if j_now == 0 and g_now + GROUPS_AHEAD < N_GROUPS:
                     load_group(g_now + GROUPS_AHEAD)
+                if i == LAG_PRODUCTS - 1:
+                    constants_on_tensor()
                 for stage, lag in stages:
                     if 0 <= i - lag < N_TILES:
                         stage(i - lag)

@@ -33,7 +33,12 @@ LAG_GATED = 9
 LAG_RESIDUAL = 13
 LAG_Y = 14
 LAG_CENTRE = 18
+LAG_INVERSE = 19
 LAG_SCALE = 23
+LAG_GAMMA = 24
+LAG_BETA = 26
+ADD_ON_VECTOR = (0, 2)
+NORM_ON_GPSIMD = (0, 2)
 GROUPS_AHEAD = 2
 
 FLOPS = 2 * 2 * TOKENS * HID * HID
@@ -106,6 +111,7 @@ def tile_crossattentionlayer_pa_t_kernel(
         nc.scalar.dma_start(out=vector_row0[0:1, 0, :], in_=ln_gamma.rearrange("(o f) -> o f", o=1))
         nc.scalar.dma_start(out=vector_row0[0:1, 1, :], in_=ln_beta.rearrange("(o f) -> o f", o=1))
         vector_rows = psum_keep.tile([P, 2, HID], BF16, name="vector_rows")
+        beta_sbuf = consts.tile([P, HID], BF16, name="beta_sbuf")
         gamma_rows = vector_rows[:, 0, :]
         beta_rows = vector_rows[:, 1, :]
 
@@ -122,6 +128,7 @@ def tile_crossattentionlayer_pa_t_kernel(
                 nc.tensor.matmul(
                     out=vector_rows[:, v, :], lhsT=ones[:], rhs=vector_row0[:, v, :], start=True, stop=True
                 )
+            nc.vector.tensor_copy(out=beta_sbuf[:], in_=beta_rows)
             bias_ps = psum.tile([P, P], F32, name="bias_ps", tag="y_ps")
             nc.tensor.transpose(bias_ps[:], bias_rows_f32[:], ident[:])
             nc.vector.tensor_copy(out=bias_cols[:], in_=bias_ps[:, 0 : 2 * CHUNKS])
@@ -218,7 +225,10 @@ def tile_crossattentionlayer_pa_t_kernel(
             )
 
         def adds_on_vector(t):
-            return t % TILES_PER_GROUP == TILES_PER_GROUP - 1
+            return t % TILES_PER_GROUP in ADD_ON_VECTOR
+
+        def on_gpsimd(t):
+            return t % TILES_PER_GROUP in NORM_ON_GPSIMD and t // TILES_PER_GROUP < N_GROUPS - 2
 
         def residual_of_tile(t):
             g, j = divmod(t, TILES_PER_GROUP)
@@ -238,7 +248,7 @@ def tile_crossattentionlayer_pa_t_kernel(
 
         def y_of_tile(t):
             g, j = divmod(t, TILES_PER_GROUP)
-            y[t] = work.tile([P, HID], F32, name="y", tag="y", bufs=10)
+            y[t] = work.tile([P, HID], F32, name="y", tag="y", bufs=13)
             if j == 0:
                 sum_y[g] = stats.tile([P, TILES_PER_GROUP], F32, name="sum_y", tag="sum_y")
             if adds_on_vector(t):
@@ -255,11 +265,12 @@ def tile_crossattentionlayer_pa_t_kernel(
                 nc.scalar.activation(
                     out=y[t][:], in_=y_ps[t][:], func=ACT.Copy, scale=1.0, accum_out=sum_y[g][:, j : j + 1]
                 )
+
+        def mean_of_group(t):
+            g, j = divmod(t, TILES_PER_GROUP)
             if j == TILES_PER_GROUP - 1:
                 neg_mean[g] = stats.tile([P, TILES_PER_GROUP], F32, name="neg_mean", tag="neg_mean")
-                nc.gpsimd.tensor_scalar(
-                    out=neg_mean[g][:], in0=sum_y[g][:], scalar1=-1.0 / HID, scalar2=None, op0=ALU.mult
-                )
+                nc.scalar.activation(out=neg_mean[g][:], in_=sum_y[g][:], func=ACT.Copy, scale=-1.0 / HID)
 
         def variance_of_tile(t):
             g, j = divmod(t, TILES_PER_GROUP)
@@ -274,6 +285,9 @@ def tile_crossattentionlayer_pa_t_kernel(
                 scale=1.0,
                 accum_out=sum_sq[g][:, j : j + 1],
             )
+
+        def inverse_of_group(t):
+            g, j = divmod(t, TILES_PER_GROUP)
             if j == TILES_PER_GROUP - 1:
                 var_eps = stats.tile([P, TILES_PER_GROUP], F32, name="var_eps", tag="var_eps")
                 nc.gpsimd.tensor_scalar(
@@ -284,6 +298,8 @@ def tile_crossattentionlayer_pa_t_kernel(
 
         def centre_tile(t):
             g, j = divmod(t, TILES_PER_GROUP)
+            if on_gpsimd(t):
+                return
             centred[t] = work.tile([P, HID], F32, name="centred", tag="centred", bufs=8)
             nc.vector.scalar_tensor_tensor(
                 out=centred[t][:],
@@ -296,7 +312,18 @@ def tile_crossattentionlayer_pa_t_kernel(
 
         def scale_tile(t):
             g, j = divmod(t, TILES_PER_GROUP)
-            result = work.tile([P, HID], F32, name="result", tag="result")
+            if on_gpsimd(t):
+                normed[t] = work.tile([P, HID], F32, name="normed", tag="normed")
+                nc.gpsimd.tensor_scalar(
+                    out=normed[t][:],
+                    in0=y[t][:],
+                    scalar1=neg_mean[g][:, j : j + 1],
+                    scalar2=rstd[g][:, j : j + 1],
+                    op0=ALU.add,
+                    op1=ALU.mult,
+                )
+                return
+            result = work.tile([P, HID], F32, name="result", tag="result", bufs=6)
             nc.vector.scalar_tensor_tensor(
                 out=result[:],
                 in0=centred[t][:],
@@ -306,6 +333,21 @@ def tile_crossattentionlayer_pa_t_kernel(
                 op1=ALU.add,
             )
             nc.sync.dma_start(out=out_dram[g][:, j, :], in_=result[:])
+
+        normed = {}
+        weighted = {}
+
+        def gamma_tile(t):
+            if on_gpsimd(t):
+                weighted[t] = work.tile([P, HID], F32, name="weighted", tag="weighted")
+                nc.vector.tensor_tensor(out=weighted[t][:], in0=normed[t][:], in1=gamma_rows, op=ALU.mult)
+
+        def beta_tile(t):
+            g, j = divmod(t, TILES_PER_GROUP)
+            if on_gpsimd(t):
+                shifted = work.tile([P, HID], F32, name="shifted", tag="shifted")
+                nc.gpsimd.tensor_tensor(out=shifted[:], in0=weighted[t][:], in1=beta_sbuf[:], op=ALU.add)
+                nc.sync.dma_start(out=out_dram[g][:, j, :], in_=shifted[:])
 
         stages = (
             (residual_of_tile, LAG_RESIDUAL),
@@ -319,9 +361,13 @@ def tile_crossattentionlayer_pa_t_kernel(
             (centre_tile, LAG_CENTRE),
             (scale_tile, LAG_SCALE),
             (quantise_tile, LAG_QUANTISE),
+            (gamma_tile, LAG_GAMMA),
+            (mean_of_group, LAG_Y),
+            (inverse_of_group, LAG_INVERSE),
+            (beta_tile, LAG_BETA),
         )
         with tc.manual_schedule():
-            for i in range(N_TILES + LAG_SCALE):
+            for i in range(N_TILES + LAG_BETA):
                 g_now, j_now = divmod(i, TILES_PER_GROUP)
                 if j_now == 0 and g_now + GROUPS_AHEAD < N_GROUPS:
                     load_group(g_now + GROUPS_AHEAD)

@@ -32,13 +32,35 @@ LAG_GATE = 8
 LAG_GATED = 9
 LAG_RESIDUAL = 13
 LAG_Y = 14
-LAG_CENTRE = 18
-LAG_INVERSE = 19
+LAG_AGGREGATE = 15
+LAG_SQUARE = 15
+LAG_EARLY_CENTRE = 15
+LAG_INVERSE = 17
+LAG_CENTRE = 22
 LAG_SCALE = 23
-LAG_GAMMA = 24
-LAG_BETA = 26
-ADD_ON_VECTOR = (0, 2)
-NORM_ON_GPSIMD = (0, 2)
+LAG_LAST = 25
+
+HEAD_ROADS = "EDAA"
+HEAD_GROUPS = 0
+ROADS = ("EDAA",)
+LAST_ROADS = "RAAA"
+LAST_GROUPS = 2
+V_COPIES = ()
+W_ROUNDS = (("wg", 3), ("wo", 4))
+
+
+def road_of(t):
+    g, j = divmod(t, TILES_PER_GROUP)
+    if g >= N_GROUPS - LAST_GROUPS:
+        return LAST_ROADS[j]
+    if g < HEAD_GROUPS:
+        return HEAD_ROADS[j]
+    return ROADS[g % len(ROADS)][j]
+
+
+Y_BANKS = 2
+Y_BUFS = 10
+CENTRED_BUFS = 8
 GROUPS_AHEAD = 2
 
 FLOPS = 2 * 2 * TOKENS * HID * HID
@@ -61,22 +83,30 @@ def tile_crossattentionlayer_pa_t_kernel(
         psum = stack.enter_context(tc.psum_pool(name="psum", bufs=2))
         psum_keep = stack.enter_context(tc.psum_pool(name="psum_keep", bufs=1))
 
-        def quantise_weight(w, label):
-            raw = consts.tile([P, PACK, HID], BF16, name=label + "_raw")
+        raw = {}
+        grouped_w = {}
+        w_codes = {}
+        w_scales = {}
+
+        def load_weight(w, label):
+            raw[label] = consts.tile([P, PACK, HID], BF16, name=label + "_raw")
             nc.sync.dma_start(
-                out=raw[:].rearrange("p (u e) f -> p u (e f)", u=2),
+                out=raw[label][:].rearrange("p (u e) f -> p u (e f)", u=2),
                 in_=w.rearrange("(u p e) f -> p u (e f)", u=2, p=P),
             )
-            grouped = consts.tile([P, HID, PACK], BF16, name=label + "_grouped", align_bytes=64)
-            nc.vector.tensor_copy(out=grouped[:], in_=raw[:].rearrange("p t f -> p f t"))
-            w_codes = consts.tile([P, HID], U32, name=label + "_codes", align_bytes=64)
-            w_scales = consts.tile([P, HID], U8, name=label + "_scales", align_bytes=64)
+
+        def group_weight(label):
+            grouped_w[label] = consts.tile([P, HID, PACK], BF16, name=label + "_grouped", align_bytes=64)
+            nc.vector.tensor_copy(out=grouped_w[label][:], in_=raw[label][:].rearrange("p t f -> p f t"))
+
+        def quantise_weight(label):
+            w_codes[label] = consts.tile([P, HID], U32, name=label + "_codes", align_bytes=64)
+            w_scales[label] = consts.tile([P, HID], U8, name=label + "_scales", align_bytes=64)
             nc.vector.quantize_mx(
-                out=w_codes[:].bitcast(FP8X4),
-                scales=w_scales[:],
-                in_=grouped[:].rearrange("p f t -> p (f t)"),
+                out=w_codes[label][:].bitcast(FP8X4),
+                scales=w_scales[label][:],
+                in_=grouped_w[label][:].rearrange("p f t -> p (f t)"),
             )
-            return w_codes, w_scales
 
         ctx_nat = {}
         hs_nat = {}
@@ -88,8 +118,8 @@ def tile_crossattentionlayer_pa_t_kernel(
             nc.sync.dma_start(out=hs_nat[g][:], in_=hs_dram[g])
 
         load_group(0)
-        wg_codes, wg_scales = quantise_weight(Wg, "wg")
-        wo_codes, wo_scales = quantise_weight(Wo, "wo")
+        load_weight(Wg, "wg")
+        load_weight(Wo, "wo")
         for g in range(1, GROUPS_AHEAD):
             load_group(g)
 
@@ -111,6 +141,7 @@ def tile_crossattentionlayer_pa_t_kernel(
         nc.scalar.dma_start(out=vector_row0[0:1, 0, :], in_=ln_gamma.rearrange("(o f) -> o f", o=1))
         nc.scalar.dma_start(out=vector_row0[0:1, 1, :], in_=ln_beta.rearrange("(o f) -> o f", o=1))
         vector_rows = psum_keep.tile([P, 2, HID], BF16, name="vector_rows")
+        gamma_sbuf = consts.tile([P, HID], BF16, name="gamma_sbuf")
         beta_sbuf = consts.tile([P, HID], BF16, name="beta_sbuf")
         gamma_rows = vector_rows[:, 0, :]
         beta_rows = vector_rows[:, 1, :]
@@ -120,14 +151,15 @@ def tile_crossattentionlayer_pa_t_kernel(
         nc.scalar.dma_start(out=bias_rows[0:CHUNKS, :], in_=bo.rearrange("(c f) -> c f", f=P))
         nc.scalar.dma_start(out=bias_rows[CHUNKS : 2 * CHUNKS, :], in_=bg.rearrange("(c f) -> c f", f=P))
         bias_rows_f32 = consts.tile([P, P], F32, name="bias_rows_f32")
-        nc.vector.tensor_copy(out=bias_rows_f32[:], in_=bias_rows[:])
         bias_cols = consts.tile([P, 2 * CHUNKS], F32, name="bias_cols")
 
         def constants_on_tensor():
+            nc.vector.tensor_copy(out=bias_rows_f32[:], in_=bias_rows[:])
             for v in range(2):
                 nc.tensor.matmul(
                     out=vector_rows[:, v, :], lhsT=ones[:], rhs=vector_row0[:, v, :], start=True, stop=True
                 )
+            nc.vector.tensor_copy(out=gamma_sbuf[:], in_=gamma_rows)
             nc.vector.tensor_copy(out=beta_sbuf[:], in_=beta_rows)
             bias_ps = psum.tile([P, P], F32, name="bias_ps", tag="y_ps")
             nc.tensor.transpose(bias_ps[:], bias_rows_f32[:], ident[:])
@@ -164,7 +196,8 @@ def tile_crossattentionlayer_pa_t_kernel(
                 grouped[g] = work.tile(
                     [P, 2, GROUP, PACK], BF16, name="grouped", tag="grouped", bufs=2, align_bytes=64
                 )
-            nc.scalar.copy(
+            copy = nc.vector.tensor_copy if t in V_COPIES else nc.scalar.copy
+            copy(
                 out=grouped[g][:].bitcast(F32)[:, :, j * P : (j + 1) * P, :],
                 in_=words_ps[t][:].rearrange("p o u r -> p o r u"),
             )
@@ -186,14 +219,14 @@ def tile_crossattentionlayer_pa_t_kernel(
             feats = slice(c * P, (c + 1) * P)
             gate_ps[s] = psum.tile([P, GROUP], F32, name="gate_ps", tag="gate_ps", bufs=1)
             attn_ps[s] = psum.tile([P, GROUP], F32, name="attn_ps", tag="attn_ps")
-            for product, w_codes, w_scales, operand in (
-                (gate_ps[s], wg_codes, wg_scales, HS),
-                (attn_ps[s], wo_codes, wo_scales, CTX),
+            for product, label, operand in (
+                (gate_ps[s], "wg", HS),
+                (attn_ps[s], "wo", CTX),
             ):
                 nc.tensor.matmul_mx(
                     out=product[:],
-                    lhsT=w_codes[:, feats].bitcast(FP8X4),
-                    lhsT_scale=w_scales[:, feats],
+                    lhsT=w_codes[label][:, feats].bitcast(FP8X4),
+                    lhsT_scale=w_scales[label][:, feats],
                     rhs=codes[g][:, operand, :].bitcast(FP8X4),
                     rhs_scale=scales[g][:, operand, :],
                     start=True,
@@ -224,16 +257,18 @@ def tile_crossattentionlayer_pa_t_kernel(
                 op1=ALU.mult,
             )
 
-        def adds_on_vector(t):
-            return t % TILES_PER_GROUP in ADD_ON_VECTOR
+        def column(t):
+            g, j = divmod(t, TILES_PER_GROUP)
+            kind = road_of(t) in "BDF"
+            return kind, sum(1 for q in range(j) if (road_of(4 * g + q) in "BDF") == kind)
 
-        def on_gpsimd(t):
-            return t % TILES_PER_GROUP in NORM_ON_GPSIMD and t // TILES_PER_GROUP < N_GROUPS - 2
+        def count(g, kind):
+            return sum(1 for q in range(TILES_PER_GROUP) if (road_of(4 * g + q) in "BDF") == kind)
 
         def residual_of_tile(t):
             g, j = divmod(t, TILES_PER_GROUP)
-            y_ps[t] = psum.tile([P, HID], F32, name="y_ps", tag="y_ps")
-            alone = adds_on_vector(t)
+            y_ps[t] = psum.tile([P, HID], F32, name="y_ps", tag="y_ps", bufs=Y_BANKS)
+            alone = road_of(t) in "ER"
             if not alone:
                 nc.tensor.matmul(out=y_ps[t][:], lhsT=ident_bf16[:], rhs=hs_nat[g][:, j, :], start=True, stop=False)
             for c in range(CHUNKS):
@@ -248,10 +283,16 @@ def tile_crossattentionlayer_pa_t_kernel(
 
         def y_of_tile(t):
             g, j = divmod(t, TILES_PER_GROUP)
-            y[t] = work.tile([P, HID], F32, name="y", tag="y", bufs=13)
-            if j == 0:
+            road = road_of(t)
+            kind, col = column(t)
+            if kind:
+                bn[t] = stats.tile([P, 6], F32, name="bn", tag="bn")
+                nc.vector.bn_stats(out=bn[t][:], in_=y_ps[t][:])
+                return
+            y[t] = work.tile([P, HID], F32, name="y", tag="y", bufs=Y_BUFS)
+            if col == 0:
                 sum_y[g] = stats.tile([P, TILES_PER_GROUP], F32, name="sum_y", tag="sum_y")
-            if adds_on_vector(t):
+            if road in "ER":
                 nc.vector.scalar_tensor_tensor(
                     out=y[t][:],
                     in0=y_ps[t][:],
@@ -259,52 +300,96 @@ def tile_crossattentionlayer_pa_t_kernel(
                     in1=hs_nat[g][:, j, :],
                     op0=ALU.mult,
                     op1=ALU.add,
-                    accum_out=sum_y[g][:, j : j + 1],
+                    accum_out=sum_y[g][:, col : col + 1],
                 )
             else:
                 nc.scalar.activation(
-                    out=y[t][:], in_=y_ps[t][:], func=ACT.Copy, scale=1.0, accum_out=sum_y[g][:, j : j + 1]
+                    out=y[t][:], in_=y_ps[t][:], func=ACT.Copy, scale=1.0, accum_out=sum_y[g][:, col : col + 1]
                 )
 
-        def mean_of_group(t):
+        def aggregate_tile(t):
             g, j = divmod(t, TILES_PER_GROUP)
-            if j == TILES_PER_GROUP - 1:
-                neg_mean[g] = stats.tile([P, TILES_PER_GROUP], F32, name="neg_mean", tag="neg_mean")
-                nc.scalar.activation(out=neg_mean[g][:], in_=sum_y[g][:], func=ACT.Copy, scale=-1.0 / HID)
+            kind, col = column(t)
+            if kind:
+                if col == 0:
+                    mean_var[g] = stats.tile([P, TILES_PER_GROUP, 2], F32, name="mean_var", tag="mean_var")
+                nc.vector.bn_aggr(out=mean_var[g][:, col, :], in_=bn[t][:])
 
-        def variance_of_tile(t):
+        def early_centre_tile(t):
             g, j = divmod(t, TILES_PER_GROUP)
+            kind, col = column(t)
+            if not kind:
+                return
+            centred[t] = work.tile([P, HID], F32, name="centred", tag="centred", bufs=CENTRED_BUFS)
+            if road_of(t) == "F":
+                nc.scalar.activation(
+                    out=centred[t][:], in_=y_ps[t][:], func=ACT.Identity, bias=mean_var[g][:, col, 0:1], scale=-1.0
+                )
+            else:
+                nc.vector.scalar_tensor_tensor(
+                    out=centred[t][:],
+                    in0=y_ps[t][:],
+                    scalar=mean_var[g][:, col, 0:1],
+                    in1=gamma_sbuf[:],
+                    op0=ALU.subtract,
+                    op1=ALU.mult,
+                )
+
+        def square_tile(t):
+            g, j = divmod(t, TILES_PER_GROUP)
+            kind, col = column(t)
+            if kind:
+                return
             squares = work.tile([P, HID], F32, name="squares", tag="squares", bufs=2)
-            if j == 0:
+            if col == 0:
                 sum_sq[g] = stats.tile([P, TILES_PER_GROUP], F32, name="sum_sq", tag="sum_sq")
             nc.scalar.activation(
                 out=squares[:],
                 in_=y[t][:],
                 func=ACT.Square,
-                bias=neg_mean[g][:, j : j + 1],
-                scale=1.0,
-                accum_out=sum_sq[g][:, j : j + 1],
+                bias=sum_y[g][:, col : col + 1],
+                scale=-float(HID),
+                accum_out=sum_sq[g][:, col : col + 1],
             )
 
         def inverse_of_group(t):
             g, j = divmod(t, TILES_PER_GROUP)
-            if j == TILES_PER_GROUP - 1:
-                var_eps = stats.tile([P, TILES_PER_GROUP], F32, name="var_eps", tag="var_eps")
+            if j < TILES_PER_GROUP - 1:
+                return
+            n = count(g, False)
+            var_eps = stats.tile([P, TILES_PER_GROUP], F32, name="var_eps", tag="var_eps")
+            if n:
+                neg_mean[g] = stats.tile([P, TILES_PER_GROUP], F32, name="neg_mean", tag="neg_mean")
                 nc.gpsimd.tensor_scalar(
-                    out=var_eps[:], in0=sum_sq[g][:], scalar1=1.0 / HID, scalar2=LN_EPS, op0=ALU.mult, op1=ALU.add
+                    out=neg_mean[g][:, 0:n], in0=sum_y[g][:, 0:n], scalar1=-1.0 / HID, scalar2=0.0, op0=ALU.mult, op1=ALU.add
                 )
-                rstd[g] = stats.tile([P, TILES_PER_GROUP], F32, name="rstd", tag="rstd")
-                nc.gpsimd.tensor_tensor(out=rstd[g][:], in0=var_eps[:], in1=neg_half[:], op=ALU.pow)
+                nc.gpsimd.tensor_scalar(
+                    out=var_eps[:, 0:n], in0=sum_sq[g][:, 0:n], scalar1=1.0 / HID**3, scalar2=LN_EPS, op0=ALU.mult, op1=ALU.add
+                )
+            if n < TILES_PER_GROUP:
+                nc.gpsimd.tensor_scalar(
+                    out=var_eps[:, n:], in0=mean_var[g][:, 0 : TILES_PER_GROUP - n, 1], scalar1=1.0, scalar2=LN_EPS, op0=ALU.mult, op1=ALU.add
+                )
+            rstd[g] = stats.tile([P, TILES_PER_GROUP], F32, name="rstd", tag="rstd")
+            nc.gpsimd.tensor_tensor(out=rstd[g][:], in0=var_eps[:], in1=neg_half[:], op=ALU.pow)
+
+        def rstd_of(t):
+            g, j = divmod(t, TILES_PER_GROUP)
+            kind, col = column(t)
+            if kind:
+                col += count(g, False)
+            return rstd[g][:, col : col + 1]
 
         def centre_tile(t):
             g, j = divmod(t, TILES_PER_GROUP)
-            if on_gpsimd(t):
+            if road_of(t) not in "AR":
                 return
-            centred[t] = work.tile([P, HID], F32, name="centred", tag="centred", bufs=8)
+            kind, col = column(t)
+            centred[t] = work.tile([P, HID], F32, name="centred", tag="centred", bufs=CENTRED_BUFS)
             nc.vector.scalar_tensor_tensor(
                 out=centred[t][:],
                 in0=y[t][:],
-                scalar=neg_mean[g][:, j : j + 1],
+                scalar=neg_mean[g][:, col : col + 1],
                 in1=gamma_rows,
                 op0=ALU.add,
                 op1=ALU.mult,
@@ -312,39 +397,53 @@ def tile_crossattentionlayer_pa_t_kernel(
 
         def scale_tile(t):
             g, j = divmod(t, TILES_PER_GROUP)
-            if on_gpsimd(t):
+            road = road_of(t)
+            kind, col = column(t)
+            if road in "DEF":
                 normed[t] = work.tile([P, HID], F32, name="normed", tag="normed")
-                nc.gpsimd.tensor_scalar(
-                    out=normed[t][:],
-                    in0=y[t][:],
-                    scalar1=neg_mean[g][:, j : j + 1],
-                    scalar2=rstd[g][:, j : j + 1],
-                    op0=ALU.add,
-                    op1=ALU.mult,
-                )
+                if road == "E":
+                    nc.gpsimd.tensor_scalar(
+                        out=normed[t][:],
+                        in0=y[t][:],
+                        scalar1=neg_mean[g][:, col : col + 1],
+                        scalar2=rstd_of(t),
+                        op0=ALU.add,
+                        op1=ALU.mult,
+                    )
+                else:
+                    nc.gpsimd.tensor_scalar(
+                        out=normed[t][:],
+                        in0=centred[t][:],
+                        scalar1=rstd_of(t),
+                        scalar2=-1.0 if road == "F" else 1.0,
+                        op0=ALU.mult,
+                        op1=ALU.mult,
+                    )
+                if road in "EF":
+                    weighted[t] = work.tile([P, HID], F32, name="weighted", tag="weighted")
+                    nc.gpsimd.tensor_tensor(out=weighted[t][:], in0=normed[t][:], in1=gamma_sbuf[:], op=ALU.mult)
+                else:
+                    weighted[t] = normed[t]
                 return
             result = work.tile([P, HID], F32, name="result", tag="result", bufs=6)
             nc.vector.scalar_tensor_tensor(
                 out=result[:],
                 in0=centred[t][:],
-                scalar=rstd[g][:, j : j + 1],
+                scalar=rstd_of(t),
                 in1=beta_rows,
                 op0=ALU.mult,
                 op1=ALU.add,
             )
             nc.sync.dma_start(out=out_dram[g][:, j, :], in_=result[:])
 
+        bn = {}
+        mean_var = {}
         normed = {}
         weighted = {}
 
-        def gamma_tile(t):
-            if on_gpsimd(t):
-                weighted[t] = work.tile([P, HID], F32, name="weighted", tag="weighted")
-                nc.vector.tensor_tensor(out=weighted[t][:], in0=normed[t][:], in1=gamma_rows, op=ALU.mult)
-
-        def beta_tile(t):
+        def last_of_tile(t):
             g, j = divmod(t, TILES_PER_GROUP)
-            if on_gpsimd(t):
+            if road_of(t) in "DEF":
                 shifted = work.tile([P, HID], F32, name="shifted", tag="shifted")
                 nc.gpsimd.tensor_tensor(out=shifted[:], in0=weighted[t][:], in1=beta_sbuf[:], op=ALU.add)
                 nc.sync.dma_start(out=out_dram[g][:, j, :], in_=shifted[:])
@@ -355,24 +454,29 @@ def tile_crossattentionlayer_pa_t_kernel(
             (products_of_chunk, LAG_PRODUCTS),
             (y_of_tile, LAG_Y),
             (gate_of_chunk, LAG_GATE),
-            (variance_of_tile, LAG_CENTRE),
+            (aggregate_tile, LAG_AGGREGATE),
             (copy_tile, LAG_COPY),
+            (square_tile, LAG_SQUARE),
             (gated_chunk, LAG_GATED),
+            (early_centre_tile, LAG_EARLY_CENTRE),
             (centre_tile, LAG_CENTRE),
             (scale_tile, LAG_SCALE),
             (quantise_tile, LAG_QUANTISE),
-            (gamma_tile, LAG_GAMMA),
-            (mean_of_group, LAG_Y),
             (inverse_of_group, LAG_INVERSE),
-            (beta_tile, LAG_BETA),
+            (last_of_tile, LAG_LAST),
         )
         with tc.manual_schedule():
-            for i in range(N_TILES + LAG_BETA):
+            for i in range(N_TILES + LAG_LAST):
                 g_now, j_now = divmod(i, TILES_PER_GROUP)
                 if j_now == 0 and g_now + GROUPS_AHEAD < N_GROUPS:
                     load_group(g_now + GROUPS_AHEAD)
                 if i == LAG_PRODUCTS - 1:
                     constants_on_tensor()
+                for label, when in W_ROUNDS:
+                    if i == when:
+                        group_weight(label)
+                    if i == when + 1:
+                        quantise_weight(label)
                 for stage, lag in stages:
                     if 0 <= i - lag < N_TILES:
                         stage(i - lag)

@@ -27,40 +27,45 @@ CTX, HS = 0, 1
 LAG_TRANSPOSE = 0
 LAG_COPY = 1
 LAG_QUANTISE = 2
-LAG_PRODUCTS = 7
-LAG_GATE = 8
-LAG_GATED = 9
-LAG_RESIDUAL = 13
-LAG_Y = 14
-LAG_AGGREGATE = 15
-LAG_SQUARE = 15
+LAG_PRODUCTS = 6
+LAG_GATE = 7
+LAG_GATED = 8
+LAG_RESIDUAL = 12
+LAG_Y = 13
+LAG_AGGREGATE = 14
+LAG_SQUARE = 14
 LAG_EARLY_CENTRE = 15
-LAG_INVERSE = 17
-LAG_CENTRE = 22
-LAG_SCALE = 23
-LAG_LAST = 25
+LAG_MOMENTS = 15
+LAG_INVERSE = 16
+LAG_CENTRE = 19
+LAG_SCALE = 20
+LAG_GPSIMD = 21
+LAG_LAST = 24
 
-HEAD_ROADS = "EDAA"
-HEAD_GROUPS = 0
-ROADS = ("EDAA",)
-LAST_ROADS = "RAAA"
-LAST_GROUPS = 2
-V_COPIES = ()
-W_ROUNDS = (("wg", 3), ("wo", 4))
+BN = "BD"
+VECTOR_ADDS = "RK"
+GPSIMD_ENDS = "JDKH"
+SCALAR_SCALES = "H"
+ROADS = ("DJAK", "DKAA")
+LAST_ROADS = "RAHA"
+LAST_GROUPS = 3
+V_COPIES = tuple(range(3, 20, 3))
+W_ROUNDS = (("wg", 0), ("wo", 1))
 
 
 def road_of(t):
     g, j = divmod(t, TILES_PER_GROUP)
     if g >= N_GROUPS - LAST_GROUPS:
         return LAST_ROADS[j]
-    if g < HEAD_GROUPS:
-        return HEAD_ROADS[j]
     return ROADS[g % len(ROADS)][j]
 
 
 Y_BANKS = 2
-Y_BUFS = 10
-CENTRED_BUFS = 8
+Y_BUFS = 12
+CENTRED_BUFS = 12
+FIRST_PIECES = (slice(0, 2), slice(2, 4))
+CONST_ROUND = 6
+LOAD_ORDER = ("wg", 0, "wo", 2)
 GROUPS_AHEAD = 2
 
 FLOPS = 2 * 2 * TOKENS * HID * HID
@@ -113,15 +118,27 @@ def tile_crossattentionlayer_pa_t_kernel(
 
         def load_group(g):
             ctx_nat[g] = loads.tile([P, TILES_PER_GROUP, HID], BF16, name="ctx_nat", tag="ctx_nat")
-            nc.sync.dma_start(out=ctx_nat[g][:], in_=ctx_dram[g])
             hs_nat[g] = loads.tile([P, TILES_PER_GROUP, HID], BF16, name="hs_nat", tag="hs_nat", bufs=7)
-            nc.sync.dma_start(out=hs_nat[g][:], in_=hs_dram[g])
+            return [
+                (nat, dram, part)
+                for part in (FIRST_PIECES if g == 0 else (slice(0, TILES_PER_GROUP),))
+                for nat, dram in ((ctx_nat[g], ctx_dram[g]), (hs_nat[g], hs_dram[g]))
+            ]
 
-        load_group(0)
-        load_weight(Wg, "wg")
-        load_weight(Wo, "wo")
+        def load_pieces(pieces):
+            for nat, dram, part in pieces:
+                nc.sync.dma_start(out=nat[:, part, :], in_=dram[:, part, :])
+
+        first = load_group(0)
+        for step in LOAD_ORDER:
+            if step == "wg":
+                load_weight(Wg, "wg")
+            elif step == "wo":
+                load_weight(Wo, "wo")
+            else:
+                load_pieces(first[step : step + 2])
         for g in range(1, GROUPS_AHEAD):
-            load_group(g)
+            load_pieces(load_group(g))
 
         table_in = consts.tile([P, 1], F32, name="table_in")
         nc.vector.memset(table_in[:], 0.0)
@@ -150,19 +167,17 @@ def tile_crossattentionlayer_pa_t_kernel(
         nc.vector.memset(bias_rows[:], 0.0)
         nc.scalar.dma_start(out=bias_rows[0:CHUNKS, :], in_=bo.rearrange("(c f) -> c f", f=P))
         nc.scalar.dma_start(out=bias_rows[CHUNKS : 2 * CHUNKS, :], in_=bg.rearrange("(c f) -> c f", f=P))
-        bias_rows_f32 = consts.tile([P, P], F32, name="bias_rows_f32")
         bias_cols = consts.tile([P, 2 * CHUNKS], F32, name="bias_cols")
 
         def constants_on_tensor():
-            nc.vector.tensor_copy(out=bias_rows_f32[:], in_=bias_rows[:])
             for v in range(2):
                 nc.tensor.matmul(
                     out=vector_rows[:, v, :], lhsT=ones[:], rhs=vector_row0[:, v, :], start=True, stop=True
                 )
             nc.vector.tensor_copy(out=gamma_sbuf[:], in_=gamma_rows)
             nc.vector.tensor_copy(out=beta_sbuf[:], in_=beta_rows)
-            bias_ps = psum.tile([P, P], F32, name="bias_ps", tag="y_ps")
-            nc.tensor.transpose(bias_ps[:], bias_rows_f32[:], ident[:])
+            bias_ps = psum.tile([P, P], BF16, name="bias_ps", tag="y_ps", bufs=Y_BANKS)
+            nc.tensor.transpose(bias_ps[:], bias_rows[:], ident_bf16[:])
             nc.vector.tensor_copy(out=bias_cols[:], in_=bias_ps[:, 0 : 2 * CHUNKS])
 
         grouped = {}
@@ -259,16 +274,16 @@ def tile_crossattentionlayer_pa_t_kernel(
 
         def column(t):
             g, j = divmod(t, TILES_PER_GROUP)
-            kind = road_of(t) in "BDF"
-            return kind, sum(1 for q in range(j) if (road_of(4 * g + q) in "BDF") == kind)
+            kind = road_of(t) in BN
+            return kind, sum(1 for q in range(j) if (road_of(4 * g + q) in BN) == kind)
 
         def count(g, kind):
-            return sum(1 for q in range(TILES_PER_GROUP) if (road_of(4 * g + q) in "BDF") == kind)
+            return sum(1 for q in range(TILES_PER_GROUP) if (road_of(4 * g + q) in BN) == kind)
 
         def residual_of_tile(t):
             g, j = divmod(t, TILES_PER_GROUP)
             y_ps[t] = psum.tile([P, HID], F32, name="y_ps", tag="y_ps", bufs=Y_BANKS)
-            alone = road_of(t) in "ER"
+            alone = road_of(t) in VECTOR_ADDS
             if not alone:
                 nc.tensor.matmul(out=y_ps[t][:], lhsT=ident_bf16[:], rhs=hs_nat[g][:, j, :], start=True, stop=False)
             for c in range(CHUNKS):
@@ -292,7 +307,7 @@ def tile_crossattentionlayer_pa_t_kernel(
             y[t] = work.tile([P, HID], F32, name="y", tag="y", bufs=Y_BUFS)
             if col == 0:
                 sum_y[g] = stats.tile([P, TILES_PER_GROUP], F32, name="sum_y", tag="sum_y")
-            if road in "ER":
+            if road in VECTOR_ADDS:
                 nc.vector.scalar_tensor_tensor(
                     out=y[t][:],
                     in0=y_ps[t][:],
@@ -321,19 +336,14 @@ def tile_crossattentionlayer_pa_t_kernel(
             if not kind:
                 return
             centred[t] = work.tile([P, HID], F32, name="centred", tag="centred", bufs=CENTRED_BUFS)
-            if road_of(t) == "F":
-                nc.scalar.activation(
-                    out=centred[t][:], in_=y_ps[t][:], func=ACT.Identity, bias=mean_var[g][:, col, 0:1], scale=-1.0
-                )
-            else:
-                nc.vector.scalar_tensor_tensor(
-                    out=centred[t][:],
-                    in0=y_ps[t][:],
-                    scalar=mean_var[g][:, col, 0:1],
-                    in1=gamma_sbuf[:],
-                    op0=ALU.subtract,
-                    op1=ALU.mult,
-                )
+            nc.vector.scalar_tensor_tensor(
+                out=centred[t][:],
+                in0=y_ps[t][:],
+                scalar=mean_var[g][:, col, 0:1],
+                in1=gamma_sbuf[:],
+                op0=ALU.subtract,
+                op1=ALU.mult,
+            )
 
         def square_tile(t):
             g, j = divmod(t, TILES_PER_GROUP)
@@ -352,26 +362,32 @@ def tile_crossattentionlayer_pa_t_kernel(
                 accum_out=sum_sq[g][:, col : col + 1],
             )
 
-        def inverse_of_group(t):
+        def moments_of_group(t):
             g, j = divmod(t, TILES_PER_GROUP)
             if j < TILES_PER_GROUP - 1:
                 return
             n = count(g, False)
-            var_eps = stats.tile([P, TILES_PER_GROUP], F32, name="var_eps", tag="var_eps")
+            var_eps[g] = stats.tile([P, TILES_PER_GROUP], F32, name="var_eps", tag="var_eps")
             if n:
                 neg_mean[g] = stats.tile([P, TILES_PER_GROUP], F32, name="neg_mean", tag="neg_mean")
-                nc.gpsimd.tensor_scalar(
-                    out=neg_mean[g][:, 0:n], in0=sum_y[g][:, 0:n], scalar1=-1.0 / HID, scalar2=0.0, op0=ALU.mult, op1=ALU.add
-                )
-                nc.gpsimd.tensor_scalar(
-                    out=var_eps[:, 0:n], in0=sum_sq[g][:, 0:n], scalar1=1.0 / HID**3, scalar2=LN_EPS, op0=ALU.mult, op1=ALU.add
+                nc.scalar.activation(out=neg_mean[g][:, 0:n], in_=sum_y[g][:, 0:n], func=ACT.Copy, scale=-1.0 / HID)
+                nc.scalar.activation(
+                    out=var_eps[g][:, 0:n], in_=sum_sq[g][:, 0:n], func=ACT.Copy, bias=LN_EPS, scale=1.0 / HID**3
                 )
             if n < TILES_PER_GROUP:
-                nc.gpsimd.tensor_scalar(
-                    out=var_eps[:, n:], in0=mean_var[g][:, 0 : TILES_PER_GROUP - n, 1], scalar1=1.0, scalar2=LN_EPS, op0=ALU.mult, op1=ALU.add
+                nc.scalar.activation(
+                    out=var_eps[g][:, n:],
+                    in_=mean_var[g][:, 0 : TILES_PER_GROUP - n, 1],
+                    func=ACT.Copy,
+                    bias=LN_EPS,
+                    scale=1.0,
                 )
-            rstd[g] = stats.tile([P, TILES_PER_GROUP], F32, name="rstd", tag="rstd")
-            nc.gpsimd.tensor_tensor(out=rstd[g][:], in0=var_eps[:], in1=neg_half[:], op=ALU.pow)
+
+        def inverse_of_group(t):
+            g, j = divmod(t, TILES_PER_GROUP)
+            if j == TILES_PER_GROUP - 1:
+                rstd[g] = stats.tile([P, TILES_PER_GROUP], F32, name="rstd", tag="rstd")
+                nc.gpsimd.tensor_tensor(out=rstd[g][:], in0=var_eps[g][:], in1=neg_half[:], op=ALU.pow)
 
         def rstd_of(t):
             g, j = divmod(t, TILES_PER_GROUP)
@@ -382,7 +398,7 @@ def tile_crossattentionlayer_pa_t_kernel(
 
         def centre_tile(t):
             g, j = divmod(t, TILES_PER_GROUP)
-            if road_of(t) not in "AR":
+            if road_of(t) in BN:
                 return
             kind, col = column(t)
             centred[t] = work.tile([P, HID], F32, name="centred", tag="centred", bufs=CENTRED_BUFS)
@@ -399,31 +415,7 @@ def tile_crossattentionlayer_pa_t_kernel(
             g, j = divmod(t, TILES_PER_GROUP)
             road = road_of(t)
             kind, col = column(t)
-            if road in "DEF":
-                normed[t] = work.tile([P, HID], F32, name="normed", tag="normed")
-                if road == "E":
-                    nc.gpsimd.tensor_scalar(
-                        out=normed[t][:],
-                        in0=y[t][:],
-                        scalar1=neg_mean[g][:, col : col + 1],
-                        scalar2=rstd_of(t),
-                        op0=ALU.add,
-                        op1=ALU.mult,
-                    )
-                else:
-                    nc.gpsimd.tensor_scalar(
-                        out=normed[t][:],
-                        in0=centred[t][:],
-                        scalar1=rstd_of(t),
-                        scalar2=-1.0 if road == "F" else 1.0,
-                        op0=ALU.mult,
-                        op1=ALU.mult,
-                    )
-                if road in "EF":
-                    weighted[t] = work.tile([P, HID], F32, name="weighted", tag="weighted")
-                    nc.gpsimd.tensor_tensor(out=weighted[t][:], in0=normed[t][:], in1=gamma_sbuf[:], op=ALU.mult)
-                else:
-                    weighted[t] = normed[t]
+            if road in GPSIMD_ENDS:
                 return
             result = work.tile([P, HID], F32, name="result", tag="result", bufs=6)
             nc.vector.scalar_tensor_tensor(
@@ -439,13 +431,23 @@ def tile_crossattentionlayer_pa_t_kernel(
         bn = {}
         mean_var = {}
         normed = {}
-        weighted = {}
+        var_eps = {}
 
-        def last_of_tile(t):
+        def gpsimd_scale_tile(t):
+            if road_of(t) in GPSIMD_ENDS:
+                normed[t] = work.tile([P, HID], F32, name="normed", tag="normed", bufs=3)
+                if road_of(t) in SCALAR_SCALES:
+                    nc.scalar.activation(out=normed[t][:], in_=centred[t][:], func=ACT.Copy, scale=rstd_of(t))
+                    return
+                nc.gpsimd.tensor_scalar(
+                    out=normed[t][:], in0=centred[t][:], scalar1=rstd_of(t), scalar2=1.0, op0=ALU.mult, op1=ALU.mult
+                )
+
+        def gpsimd_shift_tile(t):
             g, j = divmod(t, TILES_PER_GROUP)
-            if road_of(t) in "DEF":
-                shifted = work.tile([P, HID], F32, name="shifted", tag="shifted")
-                nc.gpsimd.tensor_tensor(out=shifted[:], in0=weighted[t][:], in1=beta_sbuf[:], op=ALU.add)
+            if road_of(t) in GPSIMD_ENDS:
+                shifted = work.tile([P, HID], F32, name="shifted", tag="shifted", bufs=3)
+                nc.gpsimd.tensor_tensor(out=shifted[:], in0=normed[t][:], in1=beta_sbuf[:], op=ALU.add)
                 nc.sync.dma_start(out=out_dram[g][:, j, :], in_=shifted[:])
 
         stages = (
@@ -457,20 +459,22 @@ def tile_crossattentionlayer_pa_t_kernel(
             (aggregate_tile, LAG_AGGREGATE),
             (copy_tile, LAG_COPY),
             (square_tile, LAG_SQUARE),
+            (moments_of_group, LAG_MOMENTS),
             (gated_chunk, LAG_GATED),
             (early_centre_tile, LAG_EARLY_CENTRE),
             (centre_tile, LAG_CENTRE),
             (scale_tile, LAG_SCALE),
             (quantise_tile, LAG_QUANTISE),
             (inverse_of_group, LAG_INVERSE),
-            (last_of_tile, LAG_LAST),
+            (gpsimd_shift_tile, LAG_LAST),
+            (gpsimd_scale_tile, LAG_GPSIMD),
         )
         with tc.manual_schedule():
             for i in range(N_TILES + LAG_LAST):
                 g_now, j_now = divmod(i, TILES_PER_GROUP)
                 if j_now == 0 and g_now + GROUPS_AHEAD < N_GROUPS:
-                    load_group(g_now + GROUPS_AHEAD)
-                if i == LAG_PRODUCTS - 1:
+                    load_pieces(load_group(g_now + GROUPS_AHEAD))
+                if i == CONST_ROUND:
                     constants_on_tensor()
                 for label, when in W_ROUNDS:
                     if i == when:

@@ -34,22 +34,22 @@ LAG_RESIDUAL = 12
 LAG_Y = 13
 LAG_AGGREGATE = 14
 LAG_SQUARE = 14
-LAG_EARLY_CENTRE = 15
+LAG_EARLY_CENTRE = 16
 LAG_MOMENTS = 15
 LAG_INVERSE = 16
 LAG_CENTRE = 19
-LAG_SCALE = 20
+LAG_SCALE = 21
 LAG_GPSIMD = 21
-LAG_LAST = 24
+LAG_LAST = 23
 
 BN = "BD"
 VECTOR_ADDS = "RK"
 GPSIMD_ENDS = "JDKH"
 SCALAR_SCALES = "H"
-ROADS = ("DJAK", "DKAA")
-LAST_ROADS = "RAHA"
-LAST_GROUPS = 3
-V_COPIES = tuple(range(3, 20, 3))
+ROADS = ("AKAK",)
+LAST_ROADS = "AAAA"
+LAST_GROUPS = 2
+V_COPIES = tuple(range(3, 20, 2))
 W_ROUNDS = (("wg", 0), ("wo", 1))
 
 

@@ -32,25 +32,22 @@ LAG_GATE = 7
 LAG_GATED = 8
 LAG_RESIDUAL = 12
 LAG_Y = 13
-LAG_AGGREGATE = 14
 LAG_SQUARE = 14
-LAG_EARLY_CENTRE = 16
 LAG_MOMENTS = 15
 LAG_INVERSE = 16
 LAG_CENTRE = 19
 LAG_SCALE = 21
-LAG_GPSIMD = 21
+LAG_GPSIMD = 19
 LAG_LAST = 23
 
-BN = "BD"
 VECTOR_ADDS = "RK"
 GPSIMD_ENDS = "JDKH"
 SCALAR_SCALES = "H"
-ROADS = ("AKAK",)
-LAST_ROADS = "AAAA"
+ROADS = ("KAAK",)
+LAST_ROADS = "AAHA"
 LAST_GROUPS = 2
-V_COPIES = tuple(range(3, 20, 2))
-W_ROUNDS = (("wg", 0), ("wo", 1))
+V_COPIES = tuple(range(7, 22, 2))
+W_ROUNDS = (("wg", 0), ("wo", 5))
 
 
 def road_of(t):
@@ -60,12 +57,16 @@ def road_of(t):
     return ROADS[g % len(ROADS)][j]
 
 
+ORDER = "residual transpose products y copy gate square moments gated centre scale quantise inverse shift gscale"
+HS_BUFS = 8
+GROUPED_BUFS = 3
+CODES_BUFS = 4
 Y_BANKS = 2
-Y_BUFS = 12
+Y_BUFS = 14
 CENTRED_BUFS = 12
 FIRST_PIECES = (slice(0, 2), slice(2, 4))
-CONST_ROUND = 6
-LOAD_ORDER = ("wg", 0, "wo", 2)
+CONST_ROUND = 2
+LOAD_ORDER = ("wg", 0, 1, "wo", 2, 3)
 GROUPS_AHEAD = 2
 
 FLOPS = 2 * 2 * TOKENS * HID * HID
@@ -84,7 +85,7 @@ def tile_crossattentionlayer_pa_t_kernel(
         consts = stack.enter_context(tc.tile_pool(name="consts", bufs=1))
         loads = stack.enter_context(tc.tile_pool(name="loads", bufs=4))
         work = stack.enter_context(tc.tile_pool(name="work", bufs=4))
-        stats = stack.enter_context(tc.tile_pool(name="stats", bufs=6))
+        stats = stack.enter_context(tc.tile_pool(name="stats", bufs=8))
         psum = stack.enter_context(tc.psum_pool(name="psum", bufs=2))
         psum_keep = stack.enter_context(tc.psum_pool(name="psum_keep", bufs=1))
 
@@ -118,10 +119,10 @@ def tile_crossattentionlayer_pa_t_kernel(
 
         def load_group(g):
             ctx_nat[g] = loads.tile([P, TILES_PER_GROUP, HID], BF16, name="ctx_nat", tag="ctx_nat")
-            hs_nat[g] = loads.tile([P, TILES_PER_GROUP, HID], BF16, name="hs_nat", tag="hs_nat", bufs=7)
+            hs_nat[g] = loads.tile([P, TILES_PER_GROUP, HID], BF16, name="hs_nat", tag="hs_nat", bufs=HS_BUFS)
             return [
                 (nat, dram, part)
-                for part in (FIRST_PIECES if g == 0 else (slice(0, TILES_PER_GROUP),))
+                for part in (FIRST_PIECES if g < GROUPS_AHEAD else (slice(0, TILES_PER_GROUP),))
                 for nat, dram in ((ctx_nat[g], ctx_dram[g]), (hs_nat[g], hs_dram[g]))
             ]
 
@@ -129,16 +130,14 @@ def tile_crossattentionlayer_pa_t_kernel(
             for nat, dram, part in pieces:
                 nc.sync.dma_start(out=nat[:, part, :], in_=dram[:, part, :])
 
-        first = load_group(0)
+        first = [piece for g in range(GROUPS_AHEAD) for piece in load_group(g)]
         for step in LOAD_ORDER:
             if step == "wg":
                 load_weight(Wg, "wg")
             elif step == "wo":
                 load_weight(Wo, "wo")
             else:
-                load_pieces(first[step : step + 2])
-        for g in range(1, GROUPS_AHEAD):
-            load_pieces(load_group(g))
+                load_pieces(first[2 * step : 2 * step + 2])
 
         table_in = consts.tile([P, 1], F32, name="table_in")
         nc.vector.memset(table_in[:], 0.0)
@@ -158,7 +157,6 @@ def tile_crossattentionlayer_pa_t_kernel(
         nc.scalar.dma_start(out=vector_row0[0:1, 0, :], in_=ln_gamma.rearrange("(o f) -> o f", o=1))
         nc.scalar.dma_start(out=vector_row0[0:1, 1, :], in_=ln_beta.rearrange("(o f) -> o f", o=1))
         vector_rows = psum_keep.tile([P, 2, HID], BF16, name="vector_rows")
-        gamma_sbuf = consts.tile([P, HID], BF16, name="gamma_sbuf")
         beta_sbuf = consts.tile([P, HID], BF16, name="beta_sbuf")
         gamma_rows = vector_rows[:, 0, :]
         beta_rows = vector_rows[:, 1, :]
@@ -174,7 +172,6 @@ def tile_crossattentionlayer_pa_t_kernel(
                 nc.tensor.matmul(
                     out=vector_rows[:, v, :], lhsT=ones[:], rhs=vector_row0[:, v, :], start=True, stop=True
                 )
-            nc.vector.tensor_copy(out=gamma_sbuf[:], in_=gamma_rows)
             nc.vector.tensor_copy(out=beta_sbuf[:], in_=beta_rows)
             bias_ps = psum.tile([P, P], BF16, name="bias_ps", tag="y_ps", bufs=Y_BANKS)
             nc.tensor.transpose(bias_ps[:], bias_rows[:], ident_bf16[:])
@@ -209,7 +206,7 @@ def tile_crossattentionlayer_pa_t_kernel(
             g, j = divmod(t, TILES_PER_GROUP)
             if j == 0:
                 grouped[g] = work.tile(
-                    [P, 2, GROUP, PACK], BF16, name="grouped", tag="grouped", bufs=2, align_bytes=64
+                    [P, 2, GROUP, PACK], BF16, name="grouped", tag="grouped", bufs=GROUPED_BUFS, align_bytes=64
                 )
             copy = nc.vector.tensor_copy if t in V_COPIES else nc.scalar.copy
             copy(
@@ -221,8 +218,8 @@ def tile_crossattentionlayer_pa_t_kernel(
             g, j = divmod(t, TILES_PER_GROUP)
             if j < TILES_PER_GROUP - 1:
                 return
-            codes[g] = work.tile([P, 2, GROUP], U32, name="codes", tag="codes", bufs=3, align_bytes=64)
-            scales[g] = work.tile([P, 2, GROUP], U8, name="scales", tag="scales", bufs=3, align_bytes=64)
+            codes[g] = work.tile([P, 2, GROUP], U32, name="codes", tag="codes", bufs=CODES_BUFS, align_bytes=64)
+            scales[g] = work.tile([P, 2, GROUP], U8, name="scales", tag="scales", bufs=CODES_BUFS, align_bytes=64)
             nc.vector.quantize_mx(
                 out=codes[g][:].rearrange("p o r -> p (o r)").bitcast(FP8X4),
                 scales=scales[g][:].rearrange("p o r -> p (o r)"),
@@ -272,14 +269,6 @@ def tile_crossattentionlayer_pa_t_kernel(
                 op1=ALU.mult,
             )
 
-        def column(t):
-            g, j = divmod(t, TILES_PER_GROUP)
-            kind = road_of(t) in BN
-            return kind, sum(1 for q in range(j) if (road_of(4 * g + q) in BN) == kind)
-
-        def count(g, kind):
-            return sum(1 for q in range(TILES_PER_GROUP) if (road_of(4 * g + q) in BN) == kind)
-
         def residual_of_tile(t):
             g, j = divmod(t, TILES_PER_GROUP)
             y_ps[t] = psum.tile([P, HID], F32, name="y_ps", tag="y_ps", bufs=Y_BANKS)
@@ -299,13 +288,8 @@ def tile_crossattentionlayer_pa_t_kernel(
         def y_of_tile(t):
             g, j = divmod(t, TILES_PER_GROUP)
             road = road_of(t)
-            kind, col = column(t)
-            if kind:
-                bn[t] = stats.tile([P, 6], F32, name="bn", tag="bn")
-                nc.vector.bn_stats(out=bn[t][:], in_=y_ps[t][:])
-                return
             y[t] = work.tile([P, HID], F32, name="y", tag="y", bufs=Y_BUFS)
-            if col == 0:
+            if j == 0:
                 sum_y[g] = stats.tile([P, TILES_PER_GROUP], F32, name="sum_y", tag="sum_y")
             if road in VECTOR_ADDS:
                 nc.vector.scalar_tensor_tensor(
@@ -315,73 +299,35 @@ def tile_crossattentionlayer_pa_t_kernel(
                     in1=hs_nat[g][:, j, :],
                     op0=ALU.mult,
                     op1=ALU.add,
-                    accum_out=sum_y[g][:, col : col + 1],
+                    accum_out=sum_y[g][:, j : j + 1],
                 )
             else:
                 nc.scalar.activation(
-                    out=y[t][:], in_=y_ps[t][:], func=ACT.Copy, scale=1.0, accum_out=sum_y[g][:, col : col + 1]
+                    out=y[t][:], in_=y_ps[t][:], func=ACT.Copy, scale=1.0, accum_out=sum_y[g][:, j : j + 1]
                 )
-
-        def aggregate_tile(t):
-            g, j = divmod(t, TILES_PER_GROUP)
-            kind, col = column(t)
-            if kind:
-                if col == 0:
-                    mean_var[g] = stats.tile([P, TILES_PER_GROUP, 2], F32, name="mean_var", tag="mean_var")
-                nc.vector.bn_aggr(out=mean_var[g][:, col, :], in_=bn[t][:])
-
-        def early_centre_tile(t):
-            g, j = divmod(t, TILES_PER_GROUP)
-            kind, col = column(t)
-            if not kind:
-                return
-            centred[t] = work.tile([P, HID], F32, name="centred", tag="centred", bufs=CENTRED_BUFS)
-            nc.vector.scalar_tensor_tensor(
-                out=centred[t][:],
-                in0=y_ps[t][:],
-                scalar=mean_var[g][:, col, 0:1],
-                in1=gamma_sbuf[:],
-                op0=ALU.subtract,
-                op1=ALU.mult,
-            )
 
         def square_tile(t):
             g, j = divmod(t, TILES_PER_GROUP)
-            kind, col = column(t)
-            if kind:
-                return
             squares = work.tile([P, HID], F32, name="squares", tag="squares", bufs=2)
-            if col == 0:
+            if j == 0:
                 sum_sq[g] = stats.tile([P, TILES_PER_GROUP], F32, name="sum_sq", tag="sum_sq")
             nc.scalar.activation(
                 out=squares[:],
                 in_=y[t][:],
                 func=ACT.Square,
-                bias=sum_y[g][:, col : col + 1],
+                bias=sum_y[g][:, j : j + 1],
                 scale=-float(HID),
-                accum_out=sum_sq[g][:, col : col + 1],
+                accum_out=sum_sq[g][:, j : j + 1],
             )
 
         def moments_of_group(t):
             g, j = divmod(t, TILES_PER_GROUP)
             if j < TILES_PER_GROUP - 1:
                 return
-            n = count(g, False)
+            neg_mean[g] = stats.tile([P, TILES_PER_GROUP], F32, name="neg_mean", tag="neg_mean")
+            nc.scalar.activation(out=neg_mean[g][:], in_=sum_y[g][:], func=ACT.Copy, scale=-1.0 / HID)
             var_eps[g] = stats.tile([P, TILES_PER_GROUP], F32, name="var_eps", tag="var_eps")
-            if n:
-                neg_mean[g] = stats.tile([P, TILES_PER_GROUP], F32, name="neg_mean", tag="neg_mean")
-                nc.scalar.activation(out=neg_mean[g][:, 0:n], in_=sum_y[g][:, 0:n], func=ACT.Copy, scale=-1.0 / HID)
-                nc.scalar.activation(
-                    out=var_eps[g][:, 0:n], in_=sum_sq[g][:, 0:n], func=ACT.Copy, bias=LN_EPS, scale=1.0 / HID**3
-                )
-            if n < TILES_PER_GROUP:
-                nc.scalar.activation(
-                    out=var_eps[g][:, n:],
-                    in_=mean_var[g][:, 0 : TILES_PER_GROUP - n, 1],
-                    func=ACT.Copy,
-                    bias=LN_EPS,
-                    scale=1.0,
-                )
+            nc.scalar.activation(out=var_eps[g][:], in_=sum_sq[g][:], func=ACT.Copy, bias=LN_EPS, scale=1.0 / HID**3)
 
         def inverse_of_group(t):
             g, j = divmod(t, TILES_PER_GROUP)
@@ -391,21 +337,15 @@ def tile_crossattentionlayer_pa_t_kernel(
 
         def rstd_of(t):
             g, j = divmod(t, TILES_PER_GROUP)
-            kind, col = column(t)
-            if kind:
-                col += count(g, False)
-            return rstd[g][:, col : col + 1]
+            return rstd[g][:, j : j + 1]
 
         def centre_tile(t):
             g, j = divmod(t, TILES_PER_GROUP)
-            if road_of(t) in BN:
-                return
-            kind, col = column(t)
             centred[t] = work.tile([P, HID], F32, name="centred", tag="centred", bufs=CENTRED_BUFS)
             nc.vector.scalar_tensor_tensor(
                 out=centred[t][:],
                 in0=y[t][:],
-                scalar=neg_mean[g][:, col : col + 1],
+                scalar=neg_mean[g][:, j : j + 1],
                 in1=gamma_rows,
                 op0=ALU.add,
                 op1=ALU.mult,
@@ -414,7 +354,6 @@ def tile_crossattentionlayer_pa_t_kernel(
         def scale_tile(t):
             g, j = divmod(t, TILES_PER_GROUP)
             road = road_of(t)
-            kind, col = column(t)
             if road in GPSIMD_ENDS:
                 return
             result = work.tile([P, HID], F32, name="result", tag="result", bufs=6)
@@ -428,8 +367,6 @@ def tile_crossattentionlayer_pa_t_kernel(
             )
             nc.sync.dma_start(out=out_dram[g][:, j, :], in_=result[:])
 
-        bn = {}
-        mean_var = {}
         normed = {}
         var_eps = {}
 
@@ -450,27 +387,26 @@ def tile_crossattentionlayer_pa_t_kernel(
                 nc.gpsimd.tensor_tensor(out=shifted[:], in0=normed[t][:], in1=beta_sbuf[:], op=ALU.add)
                 nc.sync.dma_start(out=out_dram[g][:, j, :], in_=shifted[:])
 
-        stages = (
-            (residual_of_tile, LAG_RESIDUAL),
-            (transpose_tile, LAG_TRANSPOSE),
-            (products_of_chunk, LAG_PRODUCTS),
-            (y_of_tile, LAG_Y),
-            (gate_of_chunk, LAG_GATE),
-            (aggregate_tile, LAG_AGGREGATE),
-            (copy_tile, LAG_COPY),
-            (square_tile, LAG_SQUARE),
-            (moments_of_group, LAG_MOMENTS),
-            (gated_chunk, LAG_GATED),
-            (early_centre_tile, LAG_EARLY_CENTRE),
-            (centre_tile, LAG_CENTRE),
-            (scale_tile, LAG_SCALE),
-            (quantise_tile, LAG_QUANTISE),
-            (inverse_of_group, LAG_INVERSE),
-            (gpsimd_shift_tile, LAG_LAST),
-            (gpsimd_scale_tile, LAG_GPSIMD),
-        )
+        stage_of = {
+            "residual": (residual_of_tile, LAG_RESIDUAL),
+            "transpose": (transpose_tile, LAG_TRANSPOSE),
+            "products": (products_of_chunk, LAG_PRODUCTS),
+            "y": (y_of_tile, LAG_Y),
+            "gate": (gate_of_chunk, LAG_GATE),
+            "copy": (copy_tile, LAG_COPY),
+            "square": (square_tile, LAG_SQUARE),
+            "moments": (moments_of_group, LAG_MOMENTS),
+            "gated": (gated_chunk, LAG_GATED),
+            "centre": (centre_tile, LAG_CENTRE),
+            "scale": (scale_tile, LAG_SCALE),
+            "quantise": (quantise_tile, LAG_QUANTISE),
+            "inverse": (inverse_of_group, LAG_INVERSE),
+            "shift": (gpsimd_shift_tile, LAG_LAST),
+            "gscale": (gpsimd_scale_tile, LAG_GPSIMD),
+        }
+        stages = [stage_of[name] for name in ORDER.split()]
         with tc.manual_schedule():
-            for i in range(N_TILES + LAG_LAST):
+            for i in range(N_TILES + max(lag for stage, lag in stages)):
                 g_now, j_now = divmod(i, TILES_PER_GROUP)
                 if j_now == 0 and g_now + GROUPS_AHEAD < N_GROUPS:
                     load_pieces(load_group(g_now + GROUPS_AHEAD))

@@ -57,7 +57,10 @@ def road_of(t):
     return ROADS[g % len(ROADS)][j]
 
 
-ORDER = "residual transpose products y copy gate square moments gated centre scale quantise inverse shift gscale"
+ORDER = "residual transpose products y gate copy square moments gated centre scale quantise inverse shift gscale"
+EARLY_GATES = 10
+LATE_GATES = 58
+LATE_Y = 54
 HS_BUFS = 8
 GROUPED_BUFS = 3
 CODES_BUFS = 4
@@ -229,7 +232,12 @@ def tile_crossattentionlayer_pa_t_kernel(
         def products_of_chunk(s):
             g, c = divmod(s, CHUNKS)
             feats = slice(c * P, (c + 1) * P)
-            gate_ps[s] = psum.tile([P, GROUP], F32, name="gate_ps", tag="gate_ps", bufs=1)
+            if s < EARLY_GATES and s % 2:
+                gate_ps[s] = psum.tile([P, GROUP], F32, name="gate_ps", tag="y_ps", bufs=Y_BANKS)
+            elif s >= LATE_GATES and s % 2:
+                gate_ps[s] = psum.tile([P, GROUP], F32, name="gate_ps", tag="words_ps")
+            else:
+                gate_ps[s] = psum.tile([P, GROUP], F32, name="gate_ps", tag="gate_ps", bufs=1)
             attn_ps[s] = psum.tile([P, GROUP], F32, name="attn_ps", tag="attn_ps")
             for product, label, operand in (
                 (gate_ps[s], "wg", HS),
@@ -271,7 +279,10 @@ def tile_crossattentionlayer_pa_t_kernel(
 
         def residual_of_tile(t):
             g, j = divmod(t, TILES_PER_GROUP)
-            y_ps[t] = psum.tile([P, HID], F32, name="y_ps", tag="y_ps", bufs=Y_BANKS)
+            if t >= LATE_Y and t % 2:
+                y_ps[t] = psum.tile([P, HID], F32, name="y_ps", tag="words_ps")
+            else:
+                y_ps[t] = psum.tile([P, HID], F32, name="y_ps", tag="y_ps", bufs=Y_BANKS)
             alone = road_of(t) in VECTOR_ADDS
             if not alone:
                 nc.tensor.matmul(out=y_ps[t][:], lhsT=ident_bf16[:], rhs=hs_nat[g][:, j, :], start=True, stop=False)

from contextlib import ExitStack

import concourse.mybir as mybir
from concourse.masks import make_identity

F32 = mybir.dt.float32
BF16 = mybir.dt.bfloat16
U32 = mybir.dt.uint32
U8 = mybir.dt.uint8
FP8X4 = mybir.dt.float8_e4m3fn_x4
ACT = mybir.ActivationFunctionType
ALU = mybir.AluOpType

P = 128
PACK = 4
HID = 512
TOKENS = 4 * 2048
LN_EPS = 1e-5

CHUNKS = HID // P
TILES_PER_GROUP = 4
GROUP = TILES_PER_GROUP * P
N_GROUPS = TOKENS // GROUP
N_TILES = TOKENS // P
CTX, HS = 0, 1

LAG_TRANSPOSE = 0
LAG_COPY = 1
LAG_QUANTISE = 2
LAG_PRODUCTS = 6
LAG_GATE = 7
LAG_GATED = 8
LAG_RESIDUAL = 12
LAG_Y = 13
LAG_SQUARE = 14
LAG_MOMENTS = 15
LAG_INVERSE = 16
LAG_CENTRE = 19
LAG_SCALE = 21
LAG_GPSIMD = 19
LAG_LAST = 23

VECTOR_ADDS = "RK"
GPSIMD_ENDS = "JDKH"
SCALAR_SCALES = "H"
ROADS = ("KAAK",)
LAST_ROADS = "AAHA"
LAST_GROUPS = 2
V_COPIES = tuple(range(7, 22, 2))
W_ROUNDS = (("wg", 0), ("wo", 5))


def road_of(t):
    g, j = divmod(t, TILES_PER_GROUP)
    if g >= N_GROUPS - LAST_GROUPS:
        return LAST_ROADS[j]
    return ROADS[g % len(ROADS)][j]


ORDER = "residual transpose products y gate copy square moments gated centre scale quantise inverse shift gscale"
EARLY_GATES = 10
LATE_GATES = 58
LATE_Y = 54
HS_BUFS = 8
GROUPED_BUFS = 3
CODES_BUFS = 4
Y_BANKS = 2
Y_BUFS = 14
CENTRED_BUFS = 12
FIRST_PIECES = (slice(0, 2), slice(2, 4))
CONST_ROUND = 2
LOAD_ORDER = ("wg", 0, 1, "wo", 2, 3)
GROUPS_AHEAD = 2

FLOPS = 2 * 2 * TOKENS * HID * HID


def tile_crossattentionlayer_pa_t_kernel(
    tc, hidden_states, attn_ctx, Wo, bo, Wg, bg, ln_gamma, ln_beta, out
):
    nc = tc.nc
    by_group = "(g p j) k -> g p j k"
    ctx_dram = attn_ctx.flatten_outer_dims().rearrange(by_group, p=P, j=TILES_PER_GROUP)
    hs_dram = hidden_states.flatten_outer_dims().rearrange(by_group, p=P, j=TILES_PER_GROUP)
    out_dram = out.flatten_outer_dims().rearrange(by_group, p=P, j=TILES_PER_GROUP)

    with ExitStack() as stack:
        consts = stack.enter_context(tc.tile_pool(name="consts", bufs=1))
        loads = stack.enter_context(tc.tile_pool(name="loads", bufs=4))
        work = stack.enter_context(tc.tile_pool(name="work", bufs=4))
        stats = stack.enter_context(tc.tile_pool(name="stats", bufs=8))
        psum = stack.enter_context(tc.psum_pool(name="psum", bufs=2))
        psum_keep = stack.enter_context(tc.psum_pool(name="psum_keep", bufs=1))

        raw = {}
        grouped_w = {}
        w_codes = {}
        w_scales = {}

        def load_weight(w, label):
            raw[label] = consts.tile([P, PACK, HID], BF16, name=label + "_raw")
            nc.sync.dma_start(
                out=raw[label][:].rearrange("p (u e) f -> p u (e f)", u=2),
                in_=w.rearrange("(u p e) f -> p u (e f)", u=2, p=P),
            )

        def group_weight(label):
            grouped_w[label] = consts.tile([P, HID, PACK], BF16, name=label + "_grouped", align_bytes=64)
            nc.vector.tensor_copy(out=grouped_w[label][:], in_=raw[label][:].rearrange("p t f -> p f t"))

        def quantise_weight(label):
            w_codes[label] = consts.tile([P, HID], U32, name=label + "_codes", align_bytes=64)
            w_scales[label] = consts.tile([P, HID], U8, name=label + "_scales", align_bytes=64)
            nc.vector.quantize_mx(
                out=w_codes[label][:].bitcast(FP8X4),
                scales=w_scales[label][:],
                in_=grouped_w[label][:].rearrange("p f t -> p (f t)"),
            )

        ctx_nat = {}
        hs_nat = {}

        def load_group(g):
            ctx_nat[g] = loads.tile([P, TILES_PER_GROUP, HID], BF16, name="ctx_nat", tag="ctx_nat")
            hs_nat[g] = loads.tile([P, TILES_PER_GROUP, HID], BF16, name="hs_nat", tag="hs_nat", bufs=HS_BUFS)
            return [
                (nat, dram, part)
                for part in (FIRST_PIECES if g < GROUPS_AHEAD else (slice(0, TILES_PER_GROUP),))
                for nat, dram in ((ctx_nat[g], ctx_dram[g]), (hs_nat[g], hs_dram[g]))
            ]

        def load_pieces(pieces):
            for nat, dram, part in pieces:
                nc.sync.dma_start(out=nat[:, part, :], in_=dram[:, part, :])

        first = [piece for g in range(GROUPS_AHEAD) for piece in load_group(g)]
        for step in LOAD_ORDER:
            if step == "wg":
                load_weight(Wg, "wg")
            elif step == "wo":
                load_weight(Wo, "wo")
            else:
                load_pieces(first[2 * step : 2 * step + 2])

        table_in = consts.tile([P, 1], F32, name="table_in")
        nc.vector.memset(table_in[:], 0.0)
        table_out = consts.tile([P, 1], F32, name="table_out")
        nc.scalar.activation(out=table_out[:], in_=table_in[:], func=ACT.Sigmoid, bias=0.0, scale=1.0)
        ident = consts.tile([P, P], F32, name="ident")
        make_identity(nc, ident[:])
        ident_bf16 = consts.tile([P, P], BF16, name="ident_bf16")
        make_identity(nc, ident_bf16[:])
        neg_half = consts.tile([P, TILES_PER_GROUP], F32, name="neg_half")
        nc.vector.memset(neg_half[:], -0.5)

        ones = consts.tile([P, P], BF16, name="ones")
        nc.vector.memset(ones[:], 1.0)
        vector_row0 = consts.tile([P, 2, HID], BF16, name="vector_row0")
        nc.vector.memset(vector_row0[:], 0.0)
        nc.scalar.dma_start(out=vector_row0[0:1, 0, :], in_=ln_gamma.rearrange("(o f) -> o f", o=1))
        nc.scalar.dma_start(out=vector_row0[0:1, 1, :], in_=ln_beta.rearrange("(o f) -> o f", o=1))
        vector_rows = psum_keep.tile([P, 2, HID], BF16, name="vector_rows")
        beta_sbuf = consts.tile([P, HID], BF16, name="beta_sbuf")
        gamma_rows = vector_rows[:, 0, :]
        beta_rows = vector_rows[:, 1, :]

        bias_rows = consts.tile([P, P], BF16, name="bias_rows")
        nc.vector.memset(bias_rows[:], 0.0)
        nc.scalar.dma_start(out=bias_rows[0:CHUNKS, :], in_=bo.rearrange("(c f) -> c f", f=P))
        nc.scalar.dma_start(out=bias_rows[CHUNKS : 2 * CHUNKS, :], in_=bg.rearrange("(c f) -> c f", f=P))
        bias_cols = consts.tile([P, 2 * CHUNKS], F32, name="bias_cols")

        def constants_on_tensor():
            for v in range(2):
                nc.tensor.matmul(
                    out=vector_rows[:, v, :], lhsT=ones[:], rhs=vector_row0[:, v, :], start=True, stop=True
                )
            nc.vector.tensor_copy(out=beta_sbuf[:], in_=beta_rows)
            bias_ps = psum.tile([P, P], BF16, name="bias_ps", tag="y_ps", bufs=Y_BANKS)
            nc.tensor.transpose(bias_ps[:], bias_rows[:], ident_bf16[:])
            nc.vector.tensor_copy(out=bias_cols[:], in_=bias_ps[:, 0 : 2 * CHUNKS])

        grouped = {}
        codes = {}
        scales = {}
        gated_t = {}
        y = {}
        centred = {}
        sum_y = {}
        neg_mean = {}
        sum_sq = {}
        rstd = {}

        words_ps = {}
        attn_ps = {}
        gate_ps = {}
        gate = {}
        y_ps = {}

        def transpose_tile(t):
            g, j = divmod(t, TILES_PER_GROUP)
            words_ps[t] = psum.tile([P, 2, 2, P], F32, name="words_ps", tag="words_ps")
            for operand, nat in ((CTX, ctx_nat[g]), (HS, hs_nat[g])):
                words = nat[:].bitcast(F32)
                for u in range(2):
                    nc.tensor.transpose(words_ps[t][:, operand, u, :], words[:, j, u * P : (u + 1) * P], ident[:])

        def copy_tile(t):
            g, j = divmod(t, TILES_PER_GROUP)
            if j == 0:
                grouped[g] = work.tile(
                    [P, 2, GROUP, PACK], BF16, name="grouped", tag="grouped", bufs=GROUPED_BUFS, align_bytes=64
                )
            copy = nc.vector.tensor_copy if t in V_COPIES else nc.scalar.copy
            copy(
                out=grouped[g][:].bitcast(F32)[:, :, j * P : (j + 1) * P, :],
                in_=words_ps[t][:].rearrange("p o u r -> p o r u"),
            )

        def quantise_tile(t):
            g, j = divmod(t, TILES_PER_GROUP)
            if j < TILES_PER_GROUP - 1:
                return
            codes[g] = work.tile([P, 2, GROUP], U32, name="codes", tag="codes", bufs=CODES_BUFS, align_bytes=64)
            scales[g] = work.tile([P, 2, GROUP], U8, name="scales", tag="scales", bufs=CODES_BUFS, align_bytes=64)
            nc.vector.quantize_mx(
                out=codes[g][:].rearrange("p o r -> p (o r)").bitcast(FP8X4),
                scales=scales[g][:].rearrange("p o r -> p (o r)"),
                in_=grouped[g][:].rearrange("p o r t -> p (o r t)"),
            )

        def products_of_chunk(s):
            g, c = divmod(s, CHUNKS)
            feats = slice(c * P, (c + 1) * P)
            if s < EARLY_GATES and s % 2:
                gate_ps[s] = psum.tile([P, GROUP], F32, name="gate_ps", tag="y_ps", bufs=Y_BANKS)
            elif s >= LATE_GATES and s % 2:
                gate_ps[s] = psum.tile([P, GROUP], F32, name="gate_ps", tag="words_ps")
            else:
                gate_ps[s] = psum.tile([P, GROUP], F32, name="gate_ps", tag="gate_ps", bufs=1)
            attn_ps[s] = psum.tile([P, GROUP], F32, name="attn_ps", tag="attn_ps")
            for product, label, operand in (
                (gate_ps[s], "wg", HS),
                (attn_ps[s], "wo", CTX),
            ):
                nc.tensor.matmul_mx(
                    out=product[:],
                    lhsT=w_codes[label][:, feats].bitcast(FP8X4),
                    lhsT_scale=w_scales[label][:, feats],
                    rhs=codes[g][:, operand, :].bitcast(FP8X4),
                    rhs_scale=scales[g][:, operand, :],
                    start=True,
                    stop=True,
                )

        def gate_of_chunk(s):
            g, c = divmod(s, CHUNKS)
            gate[s] = work.tile([P, GROUP], F32, name="gate", tag="gate")
            nc.scalar.activation(
                out=gate[s][:],
                in_=gate_ps[s][:],
                func=ACT.Sigmoid,
                bias=bias_cols[:, CHUNKS + c : CHUNKS + c + 1],
                scale=1.0,
            )

        def gated_chunk(s):
            g, c = divmod(s, CHUNKS)
            if c == 0:
                gated_t[g] = work.tile([P, CHUNKS, GROUP], F32, name="gated_t", tag="gated_t", bufs=3)
            nc.vector.scalar_tensor_tensor(
                out=gated_t[g][:, c, :],
                in0=attn_ps[s][:],
                scalar=bias_cols[:, c : c + 1],
                in1=gate[s][:],
                op0=ALU.add,
                op1=ALU.mult,
            )

        def residual_of_tile(t):
            g, j = divmod(t, TILES_PER_GROUP)
            if t >= LATE_Y and t % 2:
                y_ps[t] = psum.tile([P, HID], F32, name="y_ps", tag="words_ps")
            else:
                y_ps[t] = psum.tile([P, HID], F32, name="y_ps", tag="y_ps", bufs=Y_BANKS)
            alone = road_of(t) in VECTOR_ADDS
            if not alone:
                nc.tensor.matmul(out=y_ps[t][:], lhsT=ident_bf16[:], rhs=hs_nat[g][:, j, :], start=True, stop=False)
            for c in range(CHUNKS):
                nc.tensor.matmul(
                    out=y_ps[t][:, c * P : (c + 1) * P],
                    lhsT=gated_t[g][:, c, j * P : (j + 1) * P],
                    rhs=ident[:],
                    is_transpose=True,
                    start=alone,
                    stop=alone or c == CHUNKS - 1,
                )

        def y_of_tile(t):
            g, j = divmod(t, TILES_PER_GROUP)
            road = road_of(t)
            y[t] = work.tile([P, HID], F32, name="y", tag="y", bufs=Y_BUFS)
            if j == 0:
                sum_y[g] = stats.tile([P, TILES_PER_GROUP], F32, name="sum_y", tag="sum_y")
            if road in VECTOR_ADDS:
                nc.vector.scalar_tensor_tensor(
                    out=y[t][:],
                    in0=y_ps[t][:],
                    scalar=1.0,
                    in1=hs_nat[g][:, j, :],
                    op0=ALU.mult,
                    op1=ALU.add,
                    accum_out=sum_y[g][:, j : j + 1],
                )
            else:
                nc.scalar.activation(
                    out=y[t][:], in_=y_ps[t][:], func=ACT.Copy, scale=1.0, accum_out=sum_y[g][:, j : j + 1]
                )

        def square_tile(t):
            g, j = divmod(t, TILES_PER_GROUP)
            squares = work.tile([P, HID], F32, name="squares", tag="squares", bufs=2)
            if j == 0:
                sum_sq[g] = stats.tile([P, TILES_PER_GROUP], F32, name="sum_sq", tag="sum_sq")
            nc.scalar.activation(
                out=squares[:],
                in_=y[t][:],
                func=ACT.Square,
                bias=sum_y[g][:, j : j + 1],
                scale=-float(HID),
                accum_out=sum_sq[g][:, j : j + 1],
            )

        def moments_of_group(t):
            g, j = divmod(t, TILES_PER_GROUP)
            if j < TILES_PER_GROUP - 1:
                return
            neg_mean[g] = stats.tile([P, TILES_PER_GROUP], F32, name="neg_mean", tag="neg_mean")
            nc.scalar.activation(out=neg_mean[g][:], in_=sum_y[g][:], func=ACT.Copy, scale=-1.0 / HID)
            var_eps[g] = stats.tile([P, TILES_PER_GROUP], F32, name="var_eps", tag="var_eps")
            nc.scalar.activation(out=var_eps[g][:], in_=sum_sq[g][:], func=ACT.Copy, bias=LN_EPS, scale=1.0 / HID**3)

        def inverse_of_group(t):
            g, j = divmod(t, TILES_PER_GROUP)
            if j == TILES_PER_GROUP - 1:
                rstd[g] = stats.tile([P, TILES_PER_GROUP], F32, name="rstd", tag="rstd")
                nc.gpsimd.tensor_tensor(out=rstd[g][:], in0=var_eps[g][:], in1=neg_half[:], op=ALU.pow)

        def rstd_of(t):
            g, j = divmod(t, TILES_PER_GROUP)
            return rstd[g][:, j : j + 1]

        def centre_tile(t):
            g, j = divmod(t, TILES_PER_GROUP)
            centred[t] = work.tile([P, HID], F32, name="centred", tag="centred", bufs=CENTRED_BUFS)
            nc.vector.scalar_tensor_tensor(
                out=centred[t][:],
                in0=y[t][:],
                scalar=neg_mean[g][:, j : j + 1],
                in1=gamma_rows,
                op0=ALU.add,
                op1=ALU.mult,
            )

        def scale_tile(t):
            g, j = divmod(t, TILES_PER_GROUP)
            road = road_of(t)
            if road in GPSIMD_ENDS:
                return
            result = work.tile([P, HID], F32, name="result", tag="result", bufs=6)
            nc.vector.scalar_tensor_tensor(
                out=result[:],
                in0=centred[t][:],
                scalar=rstd_of(t),
                in1=beta_rows,
                op0=ALU.mult,
                op1=ALU.add,
            )
            nc.sync.dma_start(out=out_dram[g][:, j, :], in_=result[:])

        normed = {}
        var_eps = {}

        def gpsimd_scale_tile(t):
            if road_of(t) in GPSIMD_ENDS:
                normed[t] = work.tile([P, HID], F32, name="normed", tag="normed", bufs=3)
                if road_of(t) in SCALAR_SCALES:
                    nc.scalar.activation(out=normed[t][:], in_=centred[t][:], func=ACT.Copy, scale=rstd_of(t))
                    return
                nc.gpsimd.tensor_scalar(
                    out=normed[t][:], in0=centred[t][:], scalar1=rstd_of(t), scalar2=1.0, op0=ALU.mult, op1=ALU.mult
                )

        def gpsimd_shift_tile(t):
            g, j = divmod(t, TILES_PER_GROUP)
            if road_of(t) in GPSIMD_ENDS:
                shifted = work.tile([P, HID], F32, name="shifted", tag="shifted", bufs=3)
                nc.gpsimd.tensor_tensor(out=shifted[:], in0=normed[t][:], in1=beta_sbuf[:], op=ALU.add)
                nc.sync.dma_start(out=out_dram[g][:, j, :], in_=shifted[:])

        stage_of = {
            "residual": (residual_of_tile, LAG_RESIDUAL),
            "transpose": (transpose_tile, LAG_TRANSPOSE),
            "products": (products_of_chunk, LAG_PRODUCTS),
            "y": (y_of_tile, LAG_Y),
            "gate": (gate_of_chunk, LAG_GATE),
            "copy": (copy_tile, LAG_COPY),
            "square": (square_tile, LAG_SQUARE),
            "moments": (moments_of_group, LAG_MOMENTS),
            "gated": (gated_chunk, LAG_GATED),
            "centre": (centre_tile, LAG_CENTRE),
            "scale": (scale_tile, LAG_SCALE),
            "quantise": (quantise_tile, LAG_QUANTISE),
            "inverse": (inverse_of_group, LAG_INVERSE),
            "shift": (gpsimd_shift_tile, LAG_LAST),
            "gscale": (gpsimd_scale_tile, LAG_GPSIMD),
        }
        stages = [stage_of[name] for name in ORDER.split()]
        with tc.manual_schedule():
            for i in range(N_TILES + max(lag for stage, lag in stages)):
                g_now, j_now = divmod(i, TILES_PER_GROUP)
                if j_now == 0 and g_now + GROUPS_AHEAD < N_GROUPS:
                    load_pieces(load_group(g_now + GROUPS_AHEAD))
                if i == CONST_ROUND:
                    constants_on_tensor()
                for label, when in W_ROUNDS:
                    if i == when:
                        group_weight(label)
                    if i == when + 1:
                        quantise_weight(label)
                for stage, lag in stages:
                    if 0 <= i - lag < N_TILES:
                        stage(i - lag)
